import numpy as np
import ml_dtypes


def mxq(x, axis, fmt="e4m3"):
    dtype, down = {"e4m3": (ml_dtypes.float8_e4m3fn, 7), "e5m2": (ml_dtypes.float8_e5m2, 14)}[fmt]
    v = np.moveaxis(np.asarray(x, np.float32).astype(ml_dtypes.bfloat16).astype(np.float64), axis, -1)
    blocks = v.reshape(v.shape[:-1] + (-1, 32))
    amax = np.abs(blocks).max(-1, keepdims=True)
    byte = np.maximum(np.where(amax > 0, np.frexp(amax)[1] - 1 + 127, 0) - down, 1)
    scale = np.exp2(byte - 127.0)
    codes = (blocks / scale).astype(np.float32).astype(dtype).astype(np.float64)
    return np.moveaxis((codes * scale).reshape(v.shape), -1, axis)


WIDE = False


def mx_kscale(k):
    if not WIDE:
        return np.ones(k)
    levels = np.array([10, -10, 5, -5, 0])
    a = np.random.permutation(np.resize(levels, k // 512 * 4)).reshape(k // 512, 4)
    idx = np.arange(k)
    return np.exp2(a[idx // 512, idx % 128 // 32])


BF16 = ml_dtypes.bfloat16


def bf(x):
    return np.asarray(x, np.float32).astype(BF16)


def f64(x):
    return np.asarray(x).astype(np.float64)


E2M1 = np.array([0.0, 0.5, 1.0, 1.5, 2.0, 3.0, 4.0, 6.0, -0.0, -0.5, -1.0, -1.5, -2.0, -3.0, -4.0, -6.0])


def pack_weight(w, fmt):
    k, n = w.shape
    w = f64(bf(w)).reshape(k // 32, 32, n)
    amax = np.abs(w).max(1)
    if fmt == "e4m3":
        byte = np.frexp(amax)[1] - 1 + 127 - 7
    else:
        mant, ex = np.frexp(amax / 6.0)
        byte = np.where(mant > 0.5, ex, ex - 1) + 127
    byte = np.clip(np.where(amax > 0, byte, 1), 1, 254)
    scaled = (w * np.exp2(127.0 - byte)[:, None, :]).reshape(k, n).astype(np.float32)
    by_word = np.ascontiguousarray(scaled.reshape(k // 512, 128, 4, n).transpose(0, 1, 3, 2))
    if fmt == "e4m3":
        words = by_word.astype(ml_dtypes.float8_e4m3fn).view(np.uint8)
    else:
        c = by_word.astype(ml_dtypes.float4_e2m1fn).view(np.uint8) & 0xF
        words = c[..., 0::2] | (c[..., 1::2] << 4)
    return np.ascontiguousarray(words), np.ascontiguousarray(byte.astype(np.uint8).reshape(k // 512, 16, n))


def unpack_weight(words, scales, fmt):
    g, p, n, _ = words.shape
    if fmt == "e4m3":
        vals = np.ascontiguousarray(words).view(ml_dtypes.float8_e4m3fn).astype(np.float64)
    else:
        nib = np.empty((g, p, n, 4), np.uint8)
        nib[..., 0::2] = words & 0xF
        nib[..., 1::2] = words >> 4
        vals = E2M1[nib]
    vals = vals * np.repeat(np.exp2(scales.astype(np.float64) - 127.0), 8, axis=1)[..., None]
    return vals.transpose(0, 1, 3, 2).reshape(g * 512, n)


E, C, H, I = 4, 256, 1024, 2048
FMT = "e4m3"


def erf(z):
    z = np.clip(z, -6.0, 6.0)
    y = 2.0 * z * z
    acc = np.ones_like(z)
    for n in range(100, 0, -1):
        acc = 1.0 + acc * y / (2 * n + 1)
    return np.clip(2.0 / np.sqrt(np.pi) * z * np.exp(-z * z) * acc, -1.0, 1.0)


def gelu_erf(v):
    return 0.5 * v * (1.0 + erf(v / np.sqrt(2.0)))


def setup_inputs():
    s = mx_kscale(H)
    x = bf(np.random.standard_normal((E * C, H)) * s)
    w1 = np.random.standard_normal((E, H, I)) / np.sqrt(H) / s[:, None]
    w1_words, w1_scales = pack_weight(w1.reshape(-1, I), FMT)
    b1 = bf(np.random.standard_normal((E, I)) * 0.3)
    w2 = np.random.standard_normal((E, I, H)) * 1.5 / np.sqrt(I)
    w2_words, w2_scales = pack_weight(w2.reshape(-1, H), FMT)
    b2 = bf(np.random.standard_normal((E, H)) * 0.3)
    return {"x": x,
            "w1_words": w1_words,
            "w1_scales": w1_scales,
            "b1": b1,
            "w2_words": w2_words,
            "w2_scales": w2_scales,
            "b2": b2}


def reference(x, w1_words, w1_scales, b1, w2_words, w2_scales, b2):
    xe = f64(x).reshape(E, C, H)
    h = gelu_erf((mxq(xe, 2, "e4m3") @ unpack_weight(w1_words, w1_scales, FMT).reshape(E, H, I)) + f64(b1)[:, None, :])
    out = (mxq(h, 2, "e4m3") @ unpack_weight(w2_words, w2_scales, FMT).reshape(E, I, H)) + f64(b2)[:, None, :]
    return out.reshape(E * C, H)

@@ -1,0 +1,248 @@
+from contextlib import ExitStack
+
+import concourse.mybir as mybir
+from concourse.masks import make_identity
+
+BF16 = mybir.dt.bfloat16
+F32 = mybir.dt.float32
+I32 = mybir.dt.int32
+U32 = mybir.dt.uint32
+U8 = mybir.dt.uint8
+FP8X4 = mybir.dt.float8_e4m3fn_x4
+ADD = mybir.AluOpType.add
+GELU = mybir.ActivationFunctionType.Gelu
+
+E, C, H, I = 4, 256, 1024, 2048
+P = 128
+PACK = 4
+K_PASS = P * PACK
+N_TILE = 512
+TOK_TILES = C // P
+H_PASSES = H // K_PASS
+I_PASSES = I // K_PASS
+PAIR = 2
+W1_CHUNKS = 2
+W1_CHUNK_COLS = I // W1_CHUNKS
+PLANES = 4
+QUADRANTS = 4
+PSUM_BANKS = 8
+
+FLOPS = 2 * E * C * H * I * 2
+
+assert N_TILE == K_PASS
+
+
+def tile_fusedthorexpert_e_kernel(tc, x, w1_words, w1_scales, b1, w2_words, w2_scales, b2, out):
+    nc = tc.nc
+    with ExitStack() as ctx:
+        ctx.enter_context(tc.manual_schedule())
+        consts = ctx.enter_context(tc.tile_pool(name="consts", bufs=1))
+        x_pool = ctx.enter_context(tc.tile_pool(name="x_pool", bufs=E))
+        w1_out_pool = ctx.enter_context(tc.tile_pool(name="w1_out_pool", bufs=E * W1_CHUNKS))
+        w2_pool = ctx.enter_context(tc.tile_pool(name="w2_pool", bufs=E))
+        b1_pool = ctx.enter_context(tc.tile_pool(name="b1_pool", bufs=2))
+        b2_pool = ctx.enter_context(tc.tile_pool(name="b2_pool", bufs=3))
+        work = ctx.enter_context(tc.tile_pool(name="work", bufs=2))
+        grouped_pool = ctx.enter_context(tc.tile_pool(name="grouped_pool", bufs=3))
+        pre_pool = ctx.enter_context(tc.tile_pool(name="pre_pool", bufs=4))
+        psum = ctx.enter_context(tc.psum_pool(name="psum", bufs=PSUM_BANKS))
+
+        bias_rows = consts.tile([P, I + H], BF16)
+        nc.vector.memset(bias_rows[:].bitcast(I32), 0)
+        nc.scalar.dma_start(out=bias_rows[0:E, 0:I], in_=b1)
+        nc.scalar.dma_start(out=bias_rows[0:E, I : I + H], in_=b2)
+
+        warm_in = consts.tile([P, 1], F32)
+        warm_out = consts.tile([P, 1], F32)
+        nc.vector.memset(warm_in[:], 0.0)
+        nc.scalar.activation(out=warm_out[:], in_=warm_in[:], func=GELU)
+
+        w1_planes = consts.tile([P, E * H_PASSES // PLANES, I], U8, align_bytes=64)
+        w2_planes = consts.tile([P, E * I_PASSES // PLANES, H], U8, align_bytes=64)
+        nc.vector.memset(w1_planes[:].rearrange("p a n -> p (a n)").bitcast(I32), 0)
+        nc.vector.memset(w2_planes[:].rearrange("p a n -> p (a n)").bitcast(I32), 0)
+
+        ident_f32 = consts.tile([P, P], F32)
+        make_identity(nc, ident_f32[:])
+        ident_bf16 = consts.tile([P, P], BF16)
+        make_identity(nc, ident_bf16[:])
+
+        def load_planes(planes, scales):
+            for quadrant in range(QUADRANTS):
+                nc.sync.dma_start(
+                    out=planes[32 * quadrant : 32 * quadrant + 4 * PLANES, :].bitcast(I32),
+                    in_=scales[:, 4 * quadrant : 4 * quadrant + 4, :].bitcast(I32),
+                )
+
+        x_tiles = []
+        w1_tiles = []
+        w2_tiles = []
+
+        def load_stage1(e):
+            x_sb = x_pool.tile([P, TOK_TILES, H], BF16)
+            nc.sync.dma_start(out=x_sb[:], in_=x[C * e : C * (e + 1), :].rearrange("(p j) k -> p j k", j=TOK_TILES))
+            x_tiles.append(x_sb)
+            first_pass = H_PASSES * e
+            if first_pass % PLANES == 0:
+                a = first_pass // PLANES
+                load_planes(w1_planes[:, a, :], w1_scales[first_pass : first_pass + PLANES])
+            words = w1_words[first_pass : first_pass + H_PASSES].rearrange("g p n t -> p g (n t)")
+            chunks = []
+            for c in range(W1_CHUNKS):
+                w1_sb = w1_out_pool.tile([P, H_PASSES, W1_CHUNK_COLS], I32, tag="w1_or_out", align_bytes=64)
+                nc.sync.dma_start(
+                    out=w1_sb[:],
+                    in_=words[:, :, PACK * W1_CHUNK_COLS * c : PACK * W1_CHUNK_COLS * (c + 1)].bitcast(I32),
+                )
+                chunks.append(w1_sb)
+            w1_tiles.append(chunks)
+
+        def load_stage2(e):
+            first_pass = I_PASSES * e
+            load_planes(w2_planes[:, e, :], w2_scales[first_pass : first_pass + PLANES])
+            w2_sb = w2_pool.tile([P, I_PASSES, H], I32, align_bytes=64)
+            nc.sync.dma_start(
+                out=w2_sb[:],
+                in_=w2_words[first_pass : first_pass + I_PASSES].rearrange("g p n t -> p g (n t)").bitcast(I32),
+            )
+            w2_tiles.append(w2_sb)
+
+        load_stage1(0)
+        for e in range(E):
+            if e + 1 < E:
+                load_stage1(e + 1)
+            load_stage2(e)
+
+        b1_tiles = []
+        b2_tiles = []
+
+        def spread_biases(e):
+            pick_row = ident_bf16[:, e : e + 1].to_broadcast([P, P])
+            b1_all = b1_pool.tile([P, I], BF16)
+            b2_all = b2_pool.tile([P, H], BF16)
+            for n in range(I // N_TILE):
+                bank = psum.tile([P, N_TILE], F32, tag="bank")
+                nc.tensor.matmul(out=bank[:], lhsT=pick_row, rhs=bias_rows[:, N_TILE * n : N_TILE * (n + 1)], start=True, stop=True)
+                nc.scalar.copy(out=b1_all[:, N_TILE * n : N_TILE * (n + 1)], in_=bank[:])
+            for n in range(H // N_TILE):
+                bank = psum.tile([P, N_TILE], F32, tag="bank")
+                nc.tensor.matmul(out=bank[:], lhsT=pick_row, rhs=bias_rows[:, I + N_TILE * n : I + N_TILE * (n + 1)], start=True, stop=True)
+                nc.vector.tensor_copy(out=b2_all[:, N_TILE * n : N_TILE * (n + 1)], in_=bank[:])
+            b1_tiles.append(b1_all)
+            b2_tiles.append(b2_all)
+
+        def transpose_and_quantise(words_of, codes, scales):
+            grouped = grouped_pool.tile([P, PAIR, TOK_TILES, P, PACK], BF16, align_bytes=64)
+            for j in range(TOK_TILES):
+                bank = psum.tile([P, PAIR * 2, P], F32, tag="bank")
+                for g in range(PAIR):
+                    for u in range(2):
+                        nc.tensor.transpose(bank[:, 2 * g + u, :], words_of(j, g, u), ident_f32[:])
+                nc.scalar.copy(
+                    out=grouped[:].bitcast(F32)[:, :, j, :, :],
+                    in_=bank[:].rearrange("p (g u) w -> p g w u", u=2),
+                )
+            nc.vector.quantize_mx(
+                out=codes.bitcast(FP8X4),
+                scales=scales,
+                in_=grouped[:].rearrange("p g j w t -> p (g j w t)"),
+            )
+
+        def operand_cols(g, j):
+            first = P * (TOK_TILES * g + j)
+            return slice(first, first + P)
+
+        x_mx = []
+
+        def quantise_x(e):
+            x_words = x_tiles[e][:].bitcast(F32)
+            x_codes = work.tile([P, H_PASSES * C], U32, align_bytes=64)
+            x_scales = work.tile([P, H_PASSES * C], U8, align_bytes=64)
+            half = K_PASS // 2
+            transpose_and_quantise(
+                lambda j, g, u: x_words[:, j, half * g + u : half * (g + 1) : 2], x_codes[:], x_scales[:]
+            )
+            x_mx.append((x_codes, x_scales))
+
+        h_tiles = []
+
+        def stage1(e):
+            x_codes, x_scales = x_mx[e]
+            h_sorted = work.tile([P, TOK_TILES, I_PASSES, K_PASS], BF16)
+            for n in range(I // N_TILE):
+                w1_sb = w1_tiles[e][n * N_TILE // W1_CHUNK_COLS]
+                cols = slice(n * N_TILE % W1_CHUNK_COLS, n * N_TILE % W1_CHUNK_COLS + N_TILE)
+                for j in range(TOK_TILES):
+                    acc = psum.tile([P, N_TILE], F32, tag="bank")
+                    for g in range(H_PASSES):
+                        a, i = divmod(H_PASSES * e + g, PLANES)
+                        nc.tensor.matmul_mx(
+                            out=acc[:],
+                            lhsT=x_codes[:, operand_cols(g, j)].bitcast(FP8X4),
+                            lhsT_scale=x_scales[:, operand_cols(g, j)],
+                            rhs=w1_sb[:, g, cols].bitcast(FP8X4),
+                            rhs_scale=w1_planes[4 * i : P, a, N_TILE * n : N_TILE * (n + 1)],
+                            start=(g == 0),
+                            stop=(g == H_PASSES - 1),
+                        )
+                    pre = pre_pool.tile([P, N_TILE], F32)
+                    nc.vector.tensor_tensor(out=pre[:], in0=acc[:], in1=b1_tiles[e][:, N_TILE * n : N_TILE * (n + 1)], op=ADD)
+                    nc.scalar.activation(
+                        out=h_sorted[:, j, n, :].rearrange("p (u q v) -> p u q v", u=2, v=2),
+                        in_=pre[:].rearrange("p (q u v) -> p u q v", u=2, v=2),
+                        func=GELU,
+                    )
+            h_tiles.append(h_sorted)
+
+        h_mx = []
+
+        def quantise_h(e):
+            h_words = h_tiles[e][:].bitcast(F32)
+            h_codes = work.tile([P, I_PASSES * C], U32, align_bytes=64)
+            h_scales = work.tile([P, I_PASSES * C], U8, align_bytes=64)
+            for pair in range(I_PASSES // PAIR):
+                cols = slice(PAIR * C * pair, PAIR * C * (pair + 1))
+                transpose_and_quantise(
+                    lambda j, g, u: h_words[:, j, PAIR * pair + g, P * u : P * (u + 1)],
+                    h_codes[:, cols],
+                    h_scales[:, cols],
+                )
+            h_mx.append((h_codes, h_scales))
+
+        def stage2(e, j, out_sb):
+            h_codes, h_scales = h_mx[e]
+            for n in range(H // N_TILE):
+                cols = slice(N_TILE * n, N_TILE * (n + 1))
+                acc = psum.tile([P, N_TILE], F32, tag="bank")
+                for g in range(I_PASSES):
+                    nc.tensor.matmul_mx(
+                        out=acc[:],
+                        lhsT=h_codes[:, operand_cols(g, j)].bitcast(FP8X4),
+                        lhsT_scale=h_scales[:, operand_cols(g, j)],
+                        rhs=w2_tiles[e][:, g, cols].bitcast(FP8X4),
+                        rhs_scale=w2_planes[4 * g : P, e, cols],
+                        start=(g == 0),
+                        stop=(g == I_PASSES - 1),
+                    )
+                nc.vector.tensor_tensor(out=out_sb[:, j, cols], in0=acc[:], in1=b2_tiles[e][:, cols], op=ADD)
+            out_rows = out[C * e : C * (e + 1), :].rearrange("(p j) n -> p j n", j=TOK_TILES)
+            nc.sync.dma_start(out=out_rows[:, j, :], in_=out_sb[:, j, :])
+
+        spread_biases(0)
+        quantise_x(0)
+        spread_biases(1)
+        stage1(0)
+        quantise_x(1)
+        quantise_h(0)
+        for e in range(E):
+            if e + 1 < E:
+                stage1(e + 1)
+            if e + 2 < E:
+                spread_biases(e + 2)
+            out_sb = w1_out_pool.tile([P, TOK_TILES, H], F32, tag="w1_or_out", align_bytes=64)
+            stage2(e, 0, out_sb)
+            if e + 2 < E:
+                quantise_x(e + 2)
+            if e + 1 < E:
+                quantise_h(e + 1)
+            stage2(e, 1, out_sb)

@@ -21,8 +21,6 @@ TOK_TILES = C // P
 H_PASSES = H // K_PASS
 I_PASSES = I // K_PASS
 PAIR = 2
-W1_CHUNKS = 2
-W1_CHUNK_COLS = I // W1_CHUNKS
 PLANES = 4
 QUADRANTS = 4
 PSUM_BANKS = 8
@@ -38,11 +36,12 @@ def tile_fusedthorexpert_e_kernel(tc, x, w1_words, w1_scales, b1, w2_words, w2_s
         ctx.enter_context(tc.manual_schedule())
         consts = ctx.enter_context(tc.tile_pool(name="consts", bufs=1))
         x_pool = ctx.enter_context(tc.tile_pool(name="x_pool", bufs=E))
-        w1_out_pool = ctx.enter_context(tc.tile_pool(name="w1_out_pool", bufs=E * W1_CHUNKS))
+        w1_out_pool = ctx.enter_context(tc.tile_pool(name="w1_out_pool", bufs=E * H_PASSES))
         w2_pool = ctx.enter_context(tc.tile_pool(name="w2_pool", bufs=E))
         b1_pool = ctx.enter_context(tc.tile_pool(name="b1_pool", bufs=2))
         b2_pool = ctx.enter_context(tc.tile_pool(name="b2_pool", bufs=3))
         work = ctx.enter_context(tc.tile_pool(name="work", bufs=2))
+        sorted_pool = ctx.enter_context(tc.tile_pool(name="sorted_pool", bufs=1))
         grouped_pool = ctx.enter_context(tc.tile_pool(name="grouped_pool", bufs=3))
         pre_pool = ctx.enter_context(tc.tile_pool(name="pre_pool", bufs=4))
         psum = ctx.enter_context(tc.psum_pool(name="psum", bufs=PSUM_BANKS))
@@ -86,16 +85,12 @@ def tile_fusedthorexpert_e_kernel(tc, x, w1_words, w1_scales, b1, w2_words, w2_s
             if first_pass % PLANES == 0:
                 a = first_pass // PLANES
                 load_planes(w1_planes[:, a, :], w1_scales[first_pass : first_pass + PLANES])
-            words = w1_words[first_pass : first_pass + H_PASSES].rearrange("g p n t -> p g (n t)")
-            chunks = []
-            for c in range(W1_CHUNKS):
-                w1_sb = w1_out_pool.tile([P, H_PASSES, W1_CHUNK_COLS], I32, tag="w1_or_out", align_bytes=64)
-                nc.sync.dma_start(
-                    out=w1_sb[:],
-                    in_=words[:, :, PACK * W1_CHUNK_COLS * c : PACK * W1_CHUNK_COLS * (c + 1)].bitcast(I32),
-                )
-                chunks.append(w1_sb)
-            w1_tiles.append(chunks)
+            passes = []
+            for g in range(H_PASSES):
+                w1_sb = w1_out_pool.tile([P, I], I32, tag="w1_or_out", align_bytes=64)
+                nc.sync.dma_start(out=w1_sb[:], in_=w1_words[first_pass + g].rearrange("p n t -> p (n t)").bitcast(I32))
+                passes.append(w1_sb)
+            w1_tiles.append(passes)
 
         def load_stage2(e):
             first_pass = I_PASSES * e
@@ -152,26 +147,30 @@ def tile_fusedthorexpert_e_kernel(tc, x, w1_words, w1_scales, b1, w2_words, w2_s
             first = P * (TOK_TILES * g + j)
             return slice(first, first + P)
 
+        x_sorted_tiles = []
         x_mx = []
 
-        def quantise_x(e):
+        def sort_x(e):
             x_words = x_tiles[e][:].bitcast(F32)
+            x_sorted = sorted_pool.tile([P, TOK_TILES, H_PASSES, 2, P], F32)
+            for j in range(TOK_TILES):
+                nc.scalar.copy(out=x_sorted[:, j, :, :, :], in_=x_words[:, j, :].rearrange("p (g q u) -> p g u q", g=H_PASSES, u=2))
+            x_sorted_tiles.append(x_sorted)
+
+        def quantise_x(e):
+            x_sorted = x_sorted_tiles[e]
             x_codes = work.tile([P, H_PASSES * C], U32, align_bytes=64)
             x_scales = work.tile([P, H_PASSES * C], U8, align_bytes=64)
-            half = K_PASS // 2
-            transpose_and_quantise(
-                lambda j, g, u: x_words[:, j, half * g + u : half * (g + 1) : 2], x_codes[:], x_scales[:]
-            )
+            transpose_and_quantise(lambda j, g, u: x_sorted[:, j, g, u, :], x_codes[:], x_scales[:])
             x_mx.append((x_codes, x_scales))
 
         h_tiles = []
 
         def stage1(e):
             x_codes, x_scales = x_mx[e]
-            h_sorted = work.tile([P, TOK_TILES, I_PASSES, K_PASS], BF16)
+            h_sorted = sorted_pool.tile([P, TOK_TILES, I_PASSES, K_PASS], BF16)
             for n in range(I // N_TILE):
-                w1_sb = w1_tiles[e][n * N_TILE // W1_CHUNK_COLS]
-                cols = slice(n * N_TILE % W1_CHUNK_COLS, n * N_TILE % W1_CHUNK_COLS + N_TILE)
+                cols = slice(N_TILE * n, N_TILE * (n + 1))
                 for j in range(TOK_TILES):
                     acc = psum.tile([P, N_TILE], F32, tag="bank")
                     for g in range(H_PASSES):
@@ -180,13 +179,13 @@ def tile_fusedthorexpert_e_kernel(tc, x, w1_words, w1_scales, b1, w2_words, w2_s
                             out=acc[:],
                             lhsT=x_codes[:, operand_cols(g, j)].bitcast(FP8X4),
                             lhsT_scale=x_scales[:, operand_cols(g, j)],
-                            rhs=w1_sb[:, g, cols].bitcast(FP8X4),
-                            rhs_scale=w1_planes[4 * i : P, a, N_TILE * n : N_TILE * (n + 1)],
+                            rhs=w1_tiles[e][g][:, cols].bitcast(FP8X4),
+                            rhs_scale=w1_planes[4 * i : P, a, cols],
                             start=(g == 0),
                             stop=(g == H_PASSES - 1),
                         )
                     pre = pre_pool.tile([P, N_TILE], F32)
-                    nc.vector.tensor_tensor(out=pre[:], in0=acc[:], in1=b1_tiles[e][:, N_TILE * n : N_TILE * (n + 1)], op=ADD)
+                    nc.vector.tensor_tensor(out=pre[:], in0=acc[:], in1=b1_tiles[e][:, cols], op=ADD)
                     nc.scalar.activation(
                         out=h_sorted[:, j, n, :].rearrange("p (u q v) -> p u q v", u=2, v=2),
                         in_=pre[:].rearrange("p (q u v) -> p u q v", u=2, v=2),
@@ -228,16 +227,19 @@ def tile_fusedthorexpert_e_kernel(tc, x, w1_words, w1_scales, b1, w2_words, w2_s
             out_rows = out[C * e : C * (e + 1), :].rearrange("(p j) n -> p j n", j=TOK_TILES)
             nc.sync.dma_start(out=out_rows[:, j, :], in_=out_sb[:, j, :])
 
+        sort_x(0)
         spread_biases(0)
         quantise_x(0)
         spread_biases(1)
         stage1(0)
+        sort_x(1)
         quantise_x(1)
         quantise_h(0)
         for e in range(E):
             if e + 1 < E:
                 stage1(e + 1)
             if e + 2 < E:
+                sort_x(e + 2)
                 spread_biases(e + 2)
             out_sb = w1_out_pool.tile([P, TOK_TILES, H], F32, tag="w1_or_out", align_bytes=64)
             stage2(e, 0, out_sb)

@@ -10,6 +10,7 @@ U32 = mybir.dt.uint32
 U8 = mybir.dt.uint8
 FP8X4 = mybir.dt.float8_e4m3fn_x4
 ADD = mybir.AluOpType.add
+MULT = mybir.AluOpType.mult
 GELU = mybir.ActivationFunctionType.Gelu
 
 E, C, H, I = 4, 256, 1024, 2048
@@ -21,6 +22,8 @@ TOK_TILES = C // P
 H_PASSES = H // K_PASS
 I_PASSES = I // K_PASS
 PAIR = 2
+W1_CHUNKS = 2
+W1_CHUNK_COLS = I // W1_CHUNKS
 PLANES = 4
 QUADRANTS = 4
 PSUM_BANKS = 8
@@ -35,13 +38,14 @@ def tile_fusedthorexpert_e_kernel(tc, x, w1_words, w1_scales, b1, w2_words, w2_s
     with ExitStack() as ctx:
         ctx.enter_context(tc.manual_schedule())
         consts = ctx.enter_context(tc.tile_pool(name="consts", bufs=1))
-        x_pool = ctx.enter_context(tc.tile_pool(name="x_pool", bufs=E))
-        w1_out_pool = ctx.enter_context(tc.tile_pool(name="w1_out_pool", bufs=E * H_PASSES))
+        x_pool = ctx.enter_context(tc.tile_pool(name="x_pool", bufs=2))
+        x_sorted_pool = ctx.enter_context(tc.tile_pool(name="x_sorted_pool", bufs=E))
+        w1_out_pool = ctx.enter_context(tc.tile_pool(name="w1_out_pool", bufs=E * W1_CHUNKS))
         w2_pool = ctx.enter_context(tc.tile_pool(name="w2_pool", bufs=E))
         b1_pool = ctx.enter_context(tc.tile_pool(name="b1_pool", bufs=2))
         b2_pool = ctx.enter_context(tc.tile_pool(name="b2_pool", bufs=3))
         work = ctx.enter_context(tc.tile_pool(name="work", bufs=2))
-        sorted_pool = ctx.enter_context(tc.tile_pool(name="sorted_pool", bufs=1))
+        h_sorted_pool = ctx.enter_context(tc.tile_pool(name="h_sorted_pool", bufs=1))
         grouped_pool = ctx.enter_context(tc.tile_pool(name="grouped_pool", bufs=3))
         pre_pool = ctx.enter_context(tc.tile_pool(name="pre_pool", bufs=4))
         psum = ctx.enter_context(tc.psum_pool(name="psum", bufs=PSUM_BANKS))
@@ -73,24 +77,39 @@ def tile_fusedthorexpert_e_kernel(tc, x, w1_words, w1_scales, b1, w2_words, w2_s
                     in_=scales[:, 4 * quadrant : 4 * quadrant + 4, :].bitcast(I32),
                 )
 
-        x_tiles = []
+        x_sorted_tiles = []
         w1_tiles = []
         w2_tiles = []
 
         def load_stage1(e):
             x_sb = x_pool.tile([P, TOK_TILES, H], BF16)
             nc.sync.dma_start(out=x_sb[:], in_=x[C * e : C * (e + 1), :].rearrange("(p j) k -> p j k", j=TOK_TILES))
-            x_tiles.append(x_sb)
+            x_sorted = x_sorted_pool.tile([P, TOK_TILES, H_PASSES, K_PASS], BF16)
+            for j in range(TOK_TILES):
+                for g in range(H_PASSES):
+                    nc.gpsimd.tensor_scalar(
+                        out=x_sorted[:, j, g, :].rearrange("p (u q v) -> p u q v", u=2, v=2),
+                        in0=x_sb[:, j, K_PASS * g : K_PASS * (g + 1)].rearrange("p (q u v) -> p u q v", u=2, v=2),
+                        scalar1=1.0,
+                        scalar2=0.0,
+                        op0=MULT,
+                        op1=ADD,
+                    )
+            x_sorted_tiles.append(x_sorted)
             first_pass = H_PASSES * e
             if first_pass % PLANES == 0:
                 a = first_pass // PLANES
                 load_planes(w1_planes[:, a, :], w1_scales[first_pass : first_pass + PLANES])
-            passes = []
-            for g in range(H_PASSES):
-                w1_sb = w1_out_pool.tile([P, I], I32, tag="w1_or_out", align_bytes=64)
-                nc.sync.dma_start(out=w1_sb[:], in_=w1_words[first_pass + g].rearrange("p n t -> p (n t)").bitcast(I32))
-                passes.append(w1_sb)
-            w1_tiles.append(passes)
+            words = w1_words[first_pass : first_pass + H_PASSES].rearrange("g p n t -> p g (n t)")
+            chunks = []
+            for c in range(W1_CHUNKS):
+                w1_sb = w1_out_pool.tile([P, H_PASSES, W1_CHUNK_COLS], I32, tag="w1_or_out", align_bytes=64)
+                nc.sync.dma_start(
+                    out=w1_sb[:],
+                    in_=words[:, :, PACK * W1_CHUNK_COLS * c : PACK * W1_CHUNK_COLS * (c + 1)].bitcast(I32),
+                )
+                chunks.append(w1_sb)
+            w1_tiles.append(chunks)
 
         def load_stage2(e):
             first_pass = I_PASSES * e
@@ -115,14 +134,20 @@ def tile_fusedthorexpert_e_kernel(tc, x, w1_words, w1_scales, b1, w2_words, w2_s
             pick_row = ident_bf16[:, e : e + 1].to_broadcast([P, P])
             b1_all = b1_pool.tile([P, I], BF16)
             b2_all = b2_pool.tile([P, H], BF16)
-            for n in range(I // N_TILE):
-                bank = psum.tile([P, N_TILE], F32, tag="bank")
-                nc.tensor.matmul(out=bank[:], lhsT=pick_row, rhs=bias_rows[:, N_TILE * n : N_TILE * (n + 1)], start=True, stop=True)
-                nc.scalar.copy(out=b1_all[:, N_TILE * n : N_TILE * (n + 1)], in_=bank[:])
-            for n in range(H // N_TILE):
-                bank = psum.tile([P, N_TILE], F32, tag="bank")
-                nc.tensor.matmul(out=bank[:], lhsT=pick_row, rhs=bias_rows[:, I + N_TILE * n : I + N_TILE * (n + 1)], start=True, stop=True)
-                nc.vector.tensor_copy(out=b2_all[:, N_TILE * n : N_TILE * (n + 1)], in_=bank[:])
+            for first in range(0, I + H, 2 * N_TILE):
+                bank = psum.tile([P, 2 * N_TILE], BF16, tag="bank")
+                for half in range(2):
+                    nc.tensor.matmul(
+                        out=bank[:, N_TILE * half : N_TILE * (half + 1)],
+                        lhsT=pick_row,
+                        rhs=bias_rows[:, first + N_TILE * half : first + N_TILE * (half + 1)],
+                        start=True,
+                        stop=True,
+                    )
+                if first < I:
+                    nc.scalar.copy(out=b1_all[:, first : first + 2 * N_TILE], in_=bank[:])
+                else:
+                    nc.vector.tensor_copy(out=b2_all[:, first - I : first - I + 2 * N_TILE], in_=bank[:])
             b1_tiles.append(b1_all)
             b2_tiles.append(b2_all)
 
@@ -147,30 +172,23 @@ def tile_fusedthorexpert_e_kernel(tc, x, w1_words, w1_scales, b1, w2_words, w2_s
             first = P * (TOK_TILES * g + j)
             return slice(first, first + P)
 
-        x_sorted_tiles = []
         x_mx = []
 
-        def sort_x(e):
-            x_words = x_tiles[e][:].bitcast(F32)
-            x_sorted = sorted_pool.tile([P, TOK_TILES, H_PASSES, 2, P], F32)
-            for j in range(TOK_TILES):
-                nc.scalar.copy(out=x_sorted[:, j, :, :, :], in_=x_words[:, j, :].rearrange("p (g q u) -> p g u q", g=H_PASSES, u=2))
-            x_sorted_tiles.append(x_sorted)
-
         def quantise_x(e):
-            x_sorted = x_sorted_tiles[e]
+            x_words = x_sorted_tiles[e][:].bitcast(F32)
             x_codes = work.tile([P, H_PASSES * C], U32, align_bytes=64)
             x_scales = work.tile([P, H_PASSES * C], U8, align_bytes=64)
-            transpose_and_quantise(lambda j, g, u: x_sorted[:, j, g, u, :], x_codes[:], x_scales[:])
+            transpose_and_quantise(lambda j, g, u: x_words[:, j, g, P * u : P * (u + 1)], x_codes[:], x_scales[:])
             x_mx.append((x_codes, x_scales))
 
         h_tiles = []
 
         def stage1(e):
             x_codes, x_scales = x_mx[e]
-            h_sorted = sorted_pool.tile([P, TOK_TILES, I_PASSES, K_PASS], BF16)
+            h_sorted = h_sorted_pool.tile([P, TOK_TILES, I_PASSES, K_PASS], BF16)
             for n in range(I // N_TILE):
-                cols = slice(N_TILE * n, N_TILE * (n + 1))
+                w1_sb = w1_tiles[e][n * N_TILE // W1_CHUNK_COLS]
+                cols = slice(n * N_TILE % W1_CHUNK_COLS, n * N_TILE % W1_CHUNK_COLS + N_TILE)
                 for j in range(TOK_TILES):
                     acc = psum.tile([P, N_TILE], F32, tag="bank")
                     for g in range(H_PASSES):
@@ -179,13 +197,13 @@ def tile_fusedthorexpert_e_kernel(tc, x, w1_words, w1_scales, b1, w2_words, w2_s
                             out=acc[:],
                             lhsT=x_codes[:, operand_cols(g, j)].bitcast(FP8X4),
                             lhsT_scale=x_scales[:, operand_cols(g, j)],
-                            rhs=w1_tiles[e][g][:, cols].bitcast(FP8X4),
-                            rhs_scale=w1_planes[4 * i : P, a, cols],
+                            rhs=w1_sb[:, g, cols].bitcast(FP8X4),
+                            rhs_scale=w1_planes[4 * i : P, a, N_TILE * n : N_TILE * (n + 1)],
                             start=(g == 0),
                             stop=(g == H_PASSES - 1),
                         )
                     pre = pre_pool.tile([P, N_TILE], F32)
-                    nc.vector.tensor_tensor(out=pre[:], in0=acc[:], in1=b1_tiles[e][:, cols], op=ADD)
+                    nc.vector.tensor_tensor(out=pre[:], in0=acc[:], in1=b1_tiles[e][:, N_TILE * n : N_TILE * (n + 1)], op=ADD)
                     nc.scalar.activation(
                         out=h_sorted[:, j, n, :].rearrange("p (u q v) -> p u q v", u=2, v=2),
                         in_=pre[:].rearrange("p (q u v) -> p u q v", u=2, v=2),
@@ -210,6 +228,7 @@ def tile_fusedthorexpert_e_kernel(tc, x, w1_words, w1_scales, b1, w2_words, w2_s
 
         def stage2(e, j, out_sb):
             h_codes, h_scales = h_mx[e]
+            out_rows = out[C * e : C * (e + 1), :].rearrange("(p j) n -> p j n", j=TOK_TILES)
             for n in range(H // N_TILE):
                 cols = slice(N_TILE * n, N_TILE * (n + 1))
                 acc = psum.tile([P, N_TILE], F32, tag="bank")
@@ -224,22 +243,18 @@ def tile_fusedthorexpert_e_kernel(tc, x, w1_words, w1_scales, b1, w2_words, w2_s
                         stop=(g == I_PASSES - 1),
                     )
                 nc.vector.tensor_tensor(out=out_sb[:, j, cols], in0=acc[:], in1=b2_tiles[e][:, cols], op=ADD)
-            out_rows = out[C * e : C * (e + 1), :].rearrange("(p j) n -> p j n", j=TOK_TILES)
-            nc.sync.dma_start(out=out_rows[:, j, :], in_=out_sb[:, j, :])
+                nc.sync.dma_start(out=out_rows[:, j, cols], in_=out_sb[:, j, cols])
 
-        sort_x(0)
         spread_biases(0)
         quantise_x(0)
         spread_biases(1)
         stage1(0)
-        sort_x(1)
         quantise_x(1)
         quantise_h(0)
         for e in range(E):
             if e + 1 < E:
                 stage1(e + 1)
             if e + 2 < E:
-                sort_x(e + 2)
                 spread_biases(e + 2)
             out_sb = w1_out_pool.tile([P, TOK_TILES, H], F32, tag="w1_or_out", align_bytes=64)
             stage2(e, 0, out_sb)

@@ -10,7 +10,6 @@ U32 = mybir.dt.uint32
 U8 = mybir.dt.uint8
 FP8X4 = mybir.dt.float8_e4m3fn_x4
 ADD = mybir.AluOpType.add
-MULT = mybir.AluOpType.mult
 GELU = mybir.ActivationFunctionType.Gelu
 
 E, C, H, I = 4, 256, 1024, 2048
@@ -21,16 +20,16 @@ N_TILE = 512
 TOK_TILES = C // P
 H_PASSES = H // K_PASS
 I_PASSES = I // K_PASS
-PAIR = 2
+OUT_TILES = H // N_TILE
 W1_CHUNKS = 2
 W1_CHUNK_COLS = I // W1_CHUNKS
+W1_CHUNK_PASSES = I_PASSES // W1_CHUNKS
 PLANES = 4
 QUADRANTS = 4
 PSUM_BANKS = 8
+SCALAR_INTERLEAVES = (0, 2)
 
 FLOPS = 2 * E * C * H * I * 2
-
-assert N_TILE == K_PASS
 
 
 def tile_fusedthorexpert_e_kernel(tc, x, w1_words, w1_scales, b1, w2_words, w2_scales, b2, out):
@@ -38,37 +37,37 @@ def tile_fusedthorexpert_e_kernel(tc, x, w1_words, w1_scales, b1, w2_words, w2_s
     with ExitStack() as ctx:
         ctx.enter_context(tc.manual_schedule())
         consts = ctx.enter_context(tc.tile_pool(name="consts", bufs=1))
-        x_pool = ctx.enter_context(tc.tile_pool(name="x_pool", bufs=2))
-        x_sorted_pool = ctx.enter_context(tc.tile_pool(name="x_sorted_pool", bufs=E))
+        x_pool = ctx.enter_context(tc.tile_pool(name="x_pool", bufs=3))
         w1_out_pool = ctx.enter_context(tc.tile_pool(name="w1_out_pool", bufs=E * W1_CHUNKS))
-        w2_pool = ctx.enter_context(tc.tile_pool(name="w2_pool", bufs=E))
-        b1_pool = ctx.enter_context(tc.tile_pool(name="b1_pool", bufs=2))
-        b2_pool = ctx.enter_context(tc.tile_pool(name="b2_pool", bufs=3))
-        work = ctx.enter_context(tc.tile_pool(name="work", bufs=2))
-        h_sorted_pool = ctx.enter_context(tc.tile_pool(name="h_sorted_pool", bufs=1))
-        grouped_pool = ctx.enter_context(tc.tile_pool(name="grouped_pool", bufs=3))
-        pre_pool = ctx.enter_context(tc.tile_pool(name="pre_pool", bufs=4))
+        w1_sorted_pool = ctx.enter_context(tc.tile_pool(name="w1_sorted_pool", bufs=2 * W1_CHUNKS))
+        w2_pool = ctx.enter_context(tc.tile_pool(name="w2_pool", bufs=E * OUT_TILES))
+        x_grouped_pool = ctx.enter_context(tc.tile_pool(name="x_grouped_pool", bufs=2))
+        x_mx_pool = ctx.enter_context(tc.tile_pool(name="x_mx_pool", bufs=2))
+        h_pool = ctx.enter_context(tc.tile_pool(name="h_pool", bufs=3))
+        h_grouped_pool = ctx.enter_context(tc.tile_pool(name="h_grouped_pool", bufs=3))
+        h_mx_pool = ctx.enter_context(tc.tile_pool(name="h_mx_pool", bufs=2))
         psum = ctx.enter_context(tc.psum_pool(name="psum", bufs=PSUM_BANKS))
 
-        bias_rows = consts.tile([P, I + H], BF16)
+        w1_planes_raw = consts.tile([P, E * H_PASSES // PLANES, I], U8, align_bytes=64)
+        w1_planes = consts.tile([P, E * H_PASSES // PLANES, I], U8, align_bytes=64)
+        w2_planes = consts.tile([P, E * I_PASSES // PLANES, H], U8, align_bytes=64)
+        nc.vector.memset(w1_planes_raw[:].rearrange("p a n -> p (a n)").bitcast(I32), 0)
+
+        bias_rows = consts.tile([P, K_PASS + H], BF16)
         nc.vector.memset(bias_rows[:].bitcast(I32), 0)
-        nc.scalar.dma_start(out=bias_rows[0:E, 0:I], in_=b1)
-        nc.scalar.dma_start(out=bias_rows[0:E, I : I + H], in_=b2)
+        nc.scalar.dma_start(out=bias_rows[0 : E * I_PASSES, 0:K_PASS], in_=b1.rearrange("e (c k) -> (e c) k", k=K_PASS))
+        nc.scalar.dma_start(out=bias_rows[0:E, K_PASS : K_PASS + H], in_=b2)
+        nc.vector.memset(w2_planes[:].rearrange("p a n -> p (a n)").bitcast(I32), 0)
 
         warm_in = consts.tile([P, 1], F32)
         warm_out = consts.tile([P, 1], F32)
         nc.vector.memset(warm_in[:], 0.0)
         nc.scalar.activation(out=warm_out[:], in_=warm_in[:], func=GELU)
 
-        w1_planes = consts.tile([P, E * H_PASSES // PLANES, I], U8, align_bytes=64)
-        w2_planes = consts.tile([P, E * I_PASSES // PLANES, H], U8, align_bytes=64)
-        nc.vector.memset(w1_planes[:].rearrange("p a n -> p (a n)").bitcast(I32), 0)
-        nc.vector.memset(w2_planes[:].rearrange("p a n -> p (a n)").bitcast(I32), 0)
-
-        ident_f32 = consts.tile([P, P], F32)
-        make_identity(nc, ident_f32[:])
         ident_bf16 = consts.tile([P, P], BF16)
         make_identity(nc, ident_bf16[:])
+        ident_f32 = consts.tile([P, P], F32)
+        make_identity(nc, ident_f32[:])
 
         def load_planes(planes, scales):
             for quadrant in range(QUADRANTS):
@@ -77,189 +76,224 @@ def tile_fusedthorexpert_e_kernel(tc, x, w1_words, w1_scales, b1, w2_words, w2_s
                     in_=scales[:, 4 * quadrant : 4 * quadrant + 4, :].bitcast(I32),
                 )
 
-        x_sorted_tiles = []
-        w1_tiles = []
-        w2_tiles = []
+        x_tiles = {}
+        w1_raw_tiles = {}
+        w2_tiles = {}
 
-        def load_stage1(e):
+        def load_x(e):
             x_sb = x_pool.tile([P, TOK_TILES, H], BF16)
             nc.sync.dma_start(out=x_sb[:], in_=x[C * e : C * (e + 1), :].rearrange("(p j) k -> p j k", j=TOK_TILES))
-            x_sorted = x_sorted_pool.tile([P, TOK_TILES, H_PASSES, K_PASS], BF16)
-            for j in range(TOK_TILES):
-                for g in range(H_PASSES):
-                    nc.gpsimd.tensor_scalar(
-                        out=x_sorted[:, j, g, :].rearrange("p (u q v) -> p u q v", u=2, v=2),
-                        in0=x_sb[:, j, K_PASS * g : K_PASS * (g + 1)].rearrange("p (q u v) -> p u q v", u=2, v=2),
-                        scalar1=1.0,
-                        scalar2=0.0,
-                        op0=MULT,
-                        op1=ADD,
-                    )
-            x_sorted_tiles.append(x_sorted)
-            first_pass = H_PASSES * e
-            if first_pass % PLANES == 0:
-                a = first_pass // PLANES
-                load_planes(w1_planes[:, a, :], w1_scales[first_pass : first_pass + PLANES])
-            words = w1_words[first_pass : first_pass + H_PASSES].rearrange("g p n t -> p g (n t)")
-            chunks = []
-            for c in range(W1_CHUNKS):
-                w1_sb = w1_out_pool.tile([P, H_PASSES, W1_CHUNK_COLS], I32, tag="w1_or_out", align_bytes=64)
-                nc.sync.dma_start(
-                    out=w1_sb[:],
-                    in_=words[:, :, PACK * W1_CHUNK_COLS * c : PACK * W1_CHUNK_COLS * (c + 1)].bitcast(I32),
-                )
-                chunks.append(w1_sb)
-            w1_tiles.append(chunks)
+            x_tiles[e] = x_sb
 
-        def load_stage2(e):
-            first_pass = I_PASSES * e
-            load_planes(w2_planes[:, e, :], w2_scales[first_pass : first_pass + PLANES])
-            w2_sb = w2_pool.tile([P, I_PASSES, H], I32, align_bytes=64)
+        def load_w1(e, chunk):
+            words = w1_words[H_PASSES * e : H_PASSES * (e + 1)].rearrange("g p n t -> p g (n t)")
+            w1_raw = w1_out_pool.tile([P, H_PASSES, W1_CHUNK_COLS], I32, tag="w1_or_out", align_bytes=64)
             nc.sync.dma_start(
-                out=w2_sb[:],
-                in_=w2_words[first_pass : first_pass + I_PASSES].rearrange("g p n t -> p g (n t)").bitcast(I32),
+                out=w1_raw[:],
+                in_=words[:, :, PACK * W1_CHUNK_COLS * chunk : PACK * W1_CHUNK_COLS * (chunk + 1)].bitcast(I32),
             )
-            w2_tiles.append(w2_sb)
+            w1_raw_tiles[(e, chunk)] = w1_raw
 
-        load_stage1(0)
+        def load_w2(e, n):
+            words = w2_words[I_PASSES * e : I_PASSES * (e + 1)].rearrange("g p n t -> p g (n t)")
+            w2_sb = w2_pool.tile([P, I_PASSES, N_TILE], I32, align_bytes=64)
+            nc.sync.dma_start(out=w2_sb[:], in_=words[:, :, PACK * N_TILE * n : PACK * N_TILE * (n + 1)].bitcast(I32))
+            w2_tiles[(e, n)] = w2_sb
+
+        load_x(0)
+        for a in range(E * H_PASSES // PLANES):
+            load_planes(w1_planes_raw[:, a, :], w1_scales[PLANES * a : PLANES * (a + 1)])
+        load_w1(0, 0)
+        load_w1(0, 1)
+        load_x(1)
+        load_w1(1, 0)
+        load_w1(1, 1)
+        load_x(2)
         for e in range(E):
-            if e + 1 < E:
-                load_stage1(e + 1)
-            load_stage2(e)
+            load_planes(w2_planes[:, e, :], w2_scales[PLANES * e : PLANES * (e + 1)])
+        for e in range(E):
+            for half in range(2):
+                load_w2(e, half)
+                if e + 2 < E:
+                    load_w1(e + 2, half)
+            if e + 3 < E:
+                load_x(e + 3)
 
-        b1_tiles = []
-        b2_tiles = []
+        b1_bank = psum.tile([P, PACK, P], BF16, tag="bank")
+        for t in range(PACK):
+            nc.tensor.transpose(b1_bank[:, t, :], bias_rows[:, t:K_PASS:PACK], ident_bf16[:])
+        b1_cols = consts.tile([P, PACK, E * I_PASSES], F32)
+        nc.vector.tensor_copy(out=b1_cols[:], in_=b1_bank[:, :, 0 : E * I_PASSES])
 
-        def spread_biases(e):
+        b2_all = consts.tile([P, E, H], BF16)
+
+        def spread_b2(e):
             pick_row = ident_bf16[:, e : e + 1].to_broadcast([P, P])
-            b1_all = b1_pool.tile([P, I], BF16)
-            b2_all = b2_pool.tile([P, H], BF16)
-            for first in range(0, I + H, 2 * N_TILE):
-                bank = psum.tile([P, 2 * N_TILE], BF16, tag="bank")
-                for half in range(2):
-                    nc.tensor.matmul(
-                        out=bank[:, N_TILE * half : N_TILE * (half + 1)],
-                        lhsT=pick_row,
-                        rhs=bias_rows[:, first + N_TILE * half : first + N_TILE * (half + 1)],
-                        start=True,
-                        stop=True,
-                    )
-                if first < I:
-                    nc.scalar.copy(out=b1_all[:, first : first + 2 * N_TILE], in_=bank[:])
-                else:
-                    nc.vector.tensor_copy(out=b2_all[:, first - I : first - I + 2 * N_TILE], in_=bank[:])
-            b1_tiles.append(b1_all)
-            b2_tiles.append(b2_all)
+            bank = psum.tile([P, H], BF16, tag="bank")
+            for n in range(OUT_TILES):
+                nc.tensor.matmul(
+                    out=bank[:, N_TILE * n : N_TILE * (n + 1)],
+                    lhsT=pick_row,
+                    rhs=bias_rows[:, K_PASS + N_TILE * n : K_PASS + N_TILE * (n + 1)],
+                    start=True,
+                    stop=True,
+                )
+            nc.scalar.copy(out=b2_all[:, e, :], in_=bank[:])
 
-        def transpose_and_quantise(words_of, codes, scales):
-            grouped = grouped_pool.tile([P, PAIR, TOK_TILES, P, PACK], BF16, align_bytes=64)
+        def sort_planes(a):
+            for t in range(PACK):
+                nc.vector.tensor_copy(
+                    out=w1_planes[:, a, :].rearrange("p (c t m) -> p t c m", t=PACK, m=P)[:, t],
+                    in_=w1_planes_raw[:, a, :].rearrange("p (c m t) -> p t c m", t=PACK, m=P)[:, t],
+                )
+
+        w1_sorted_tiles = {}
+
+        def sort_w1(e, chunk):
+            w1_sorted = w1_sorted_pool.tile([P, H_PASSES, W1_CHUNK_COLS], I32, align_bytes=64)
+            nc.vector.tensor_copy(
+                out=w1_sorted[:].rearrange("p g n -> p (g n)").rearrange("p (c t m) -> p c t m", t=PACK, m=P),
+                in_=w1_raw_tiles[(e, chunk)][:].rearrange("p g n -> p (g n)").rearrange("p (c m t) -> p c t m", t=PACK, m=P),
+            )
+            w1_sorted_tiles[(e, chunk)] = w1_sorted
+
+        x_grouped_tiles = {}
+        x_mx = {}
+
+        def transpose_x(e):
+            x_words = x_tiles[e][:].bitcast(F32)
+            grouped = x_grouped_pool.tile([P, H_PASSES, TOK_TILES, P, PACK], BF16, align_bytes=64)
             for j in range(TOK_TILES):
-                bank = psum.tile([P, PAIR * 2, P], F32, tag="bank")
-                for g in range(PAIR):
+                bank = psum.tile([P, H_PASSES * 2, P], F32, tag="bank")
+                for g in range(H_PASSES):
                     for u in range(2):
-                        nc.tensor.transpose(bank[:, 2 * g + u, :], words_of(j, g, u), ident_f32[:])
+                        first = K_PASS // 2 * g
+                        nc.tensor.transpose(bank[:, 2 * g + u, :], x_words[:, j, first + u : first + K_PASS // 2 : 2], ident_f32[:])
                 nc.scalar.copy(
                     out=grouped[:].bitcast(F32)[:, :, j, :, :],
                     in_=bank[:].rearrange("p (g u) w -> p g w u", u=2),
                 )
-            nc.vector.quantize_mx(
-                out=codes.bitcast(FP8X4),
-                scales=scales,
-                in_=grouped[:].rearrange("p g j w t -> p (g j w t)"),
-            )
-
-        def operand_cols(g, j):
-            first = P * (TOK_TILES * g + j)
-            return slice(first, first + P)
-
-        x_mx = []
+            x_grouped_tiles[e] = grouped
 
         def quantise_x(e):
-            x_words = x_sorted_tiles[e][:].bitcast(F32)
-            x_codes = work.tile([P, H_PASSES * C], U32, align_bytes=64)
-            x_scales = work.tile([P, H_PASSES * C], U8, align_bytes=64)
-            transpose_and_quantise(lambda j, g, u: x_words[:, j, g, P * u : P * (u + 1)], x_codes[:], x_scales[:])
-            x_mx.append((x_codes, x_scales))
+            x_codes = x_mx_pool.tile([P, H_PASSES * C], U32, align_bytes=64)
+            x_scales = x_mx_pool.tile([P, H_PASSES * C], U8, align_bytes=64)
+            nc.vector.quantize_mx(
+                out=x_codes[:].bitcast(FP8X4),
+                scales=x_scales[:],
+                in_=x_grouped_tiles[e][:].rearrange("p g j w t -> p (g j w t)"),
+            )
+            x_mx[e] = (x_codes, x_scales)
 
-        h_tiles = []
+        h_tiles = {}
 
-        def stage1(e):
+        def stage1(e, c):
             x_codes, x_scales = x_mx[e]
-            h_sorted = h_sorted_pool.tile([P, TOK_TILES, I_PASSES, K_PASS], BF16)
-            for n in range(I // N_TILE):
-                w1_sb = w1_tiles[e][n * N_TILE // W1_CHUNK_COLS]
-                cols = slice(n * N_TILE % W1_CHUNK_COLS, n * N_TILE % W1_CHUNK_COLS + N_TILE)
-                for j in range(TOK_TILES):
-                    acc = psum.tile([P, N_TILE], F32, tag="bank")
+            w1_sorted = w1_sorted_tiles[(e, c // W1_CHUNK_PASSES)]
+            h_rows = h_pool.tile([P, PACK, C], BF16)
+            for half in range(2):
+                bank = psum.tile([P, 2, C], F32, tag="bank")
+                for s in range(2):
+                    t = 2 * half + s
+                    first = K_PASS * (c % W1_CHUNK_PASSES) + P * t
                     for g in range(H_PASSES):
                         a, i = divmod(H_PASSES * e + g, PLANES)
                         nc.tensor.matmul_mx(
-                            out=acc[:],
-                            lhsT=x_codes[:, operand_cols(g, j)].bitcast(FP8X4),
-                            lhsT_scale=x_scales[:, operand_cols(g, j)],
-                            rhs=w1_sb[:, g, cols].bitcast(FP8X4),
-                            rhs_scale=w1_planes[4 * i : P, a, N_TILE * n : N_TILE * (n + 1)],
+                            out=bank[:, s, :],
+                            lhsT=w1_sorted[:, g, first : first + P].bitcast(FP8X4),
+                            lhsT_scale=w1_planes[4 * i : P, a, K_PASS * c + P * t : K_PASS * c + P * (t + 1)],
+                            rhs=x_codes[:, C * g : C * (g + 1)].bitcast(FP8X4),
+                            rhs_scale=x_scales[:, C * g : C * (g + 1)],
                             start=(g == 0),
                             stop=(g == H_PASSES - 1),
                         )
-                    pre = pre_pool.tile([P, N_TILE], F32)
-                    nc.vector.tensor_tensor(out=pre[:], in0=acc[:], in1=b1_tiles[e][:, N_TILE * n : N_TILE * (n + 1)], op=ADD)
+                for s in range(2):
+                    t = 2 * half + s
                     nc.scalar.activation(
-                        out=h_sorted[:, j, n, :].rearrange("p (u q v) -> p u q v", u=2, v=2),
-                        in_=pre[:].rearrange("p (q u v) -> p u q v", u=2, v=2),
+                        out=h_rows[:, t, :],
+                        in_=bank[:, s, :],
                         func=GELU,
+                        bias=b1_cols[:, t, I_PASSES * e + c : I_PASSES * e + c + 1],
                     )
-            h_tiles.append(h_sorted)
+            h_tiles[(e, c)] = h_rows
 
-        h_mx = []
+        h_grouped_tiles = {}
+        h_mx = {}
 
-        def quantise_h(e):
-            h_words = h_tiles[e][:].bitcast(F32)
-            h_codes = work.tile([P, I_PASSES * C], U32, align_bytes=64)
-            h_scales = work.tile([P, I_PASSES * C], U8, align_bytes=64)
-            for pair in range(I_PASSES // PAIR):
-                cols = slice(PAIR * C * pair, PAIR * C * (pair + 1))
-                transpose_and_quantise(
-                    lambda j, g, u: h_words[:, j, PAIR * pair + g, P * u : P * (u + 1)],
-                    h_codes[:, cols],
-                    h_scales[:, cols],
-                )
-            h_mx.append((h_codes, h_scales))
+        def interleave_h(e, c):
+            grouped = h_grouped_pool.tile([P, C, PACK], BF16, align_bytes=64)
+            if c in SCALAR_INTERLEAVES:
+                nc.scalar.copy(out=grouped[:], in_=h_tiles[(e, c)][:].rearrange("p t w -> p w t"))
+            else:
+                nc.vector.tensor_copy(out=grouped[:], in_=h_tiles[(e, c)][:].rearrange("p t w -> p w t"))
+            h_grouped_tiles[(e, c)] = grouped
 
-        def stage2(e, j, out_sb):
+        def quantise_h(e, c):
+            if c == 0:
+                h_codes = h_mx_pool.tile([P, I_PASSES * C], U32, align_bytes=64)
+                h_scales = h_mx_pool.tile([P, I_PASSES * C], U8, align_bytes=64)
+                h_mx[e] = (h_codes, h_scales)
+            h_codes, h_scales = h_mx[e]
+            nc.vector.quantize_mx(
+                out=h_codes[:, C * c : C * (c + 1)].bitcast(FP8X4),
+                scales=h_scales[:, C * c : C * (c + 1)],
+                in_=h_grouped_tiles[(e, c)][:].rearrange("p w t -> p (w t)"),
+            )
+
+        out_tiles = {}
+
+        def stage2(e, j, n):
+            if e not in out_tiles:
+                out_sb = w1_out_pool.tile([P, TOK_TILES, H], F32, tag="w1_or_out", align_bytes=64)
+                out_tiles[e] = out_sb
+            out_sb = out_tiles[e]
             h_codes, h_scales = h_mx[e]
             out_rows = out[C * e : C * (e + 1), :].rearrange("(p j) n -> p j n", j=TOK_TILES)
-            for n in range(H // N_TILE):
-                cols = slice(N_TILE * n, N_TILE * (n + 1))
-                acc = psum.tile([P, N_TILE], F32, tag="bank")
-                for g in range(I_PASSES):
-                    nc.tensor.matmul_mx(
-                        out=acc[:],
-                        lhsT=h_codes[:, operand_cols(g, j)].bitcast(FP8X4),
-                        lhsT_scale=h_scales[:, operand_cols(g, j)],
-                        rhs=w2_tiles[e][:, g, cols].bitcast(FP8X4),
-                        rhs_scale=w2_planes[4 * g : P, e, cols],
-                        start=(g == 0),
-                        stop=(g == I_PASSES - 1),
-                    )
-                nc.vector.tensor_tensor(out=out_sb[:, j, cols], in0=acc[:], in1=b2_tiles[e][:, cols], op=ADD)
-                nc.sync.dma_start(out=out_rows[:, j, cols], in_=out_sb[:, j, cols])
+            cols = slice(N_TILE * n, N_TILE * (n + 1))
+            acc = psum.tile([P, N_TILE], F32, tag="bank")
+            for c in range(I_PASSES):
+                tokens = slice(C * c + P * j, C * c + P * (j + 1))
+                nc.tensor.matmul_mx(
+                    out=acc[:],
+                    lhsT=h_codes[:, tokens].bitcast(FP8X4),
+                    lhsT_scale=h_scales[:, tokens],
+                    rhs=w2_tiles[(e, n)][:, c, :].bitcast(FP8X4),
+                    rhs_scale=w2_planes[4 * c : P, e, cols],
+                    start=(c == 0),
+                    stop=(c == I_PASSES - 1),
+                )
+            nc.vector.tensor_tensor(out=out_sb[:, j, cols], in0=acc[:], in1=b2_all[:, e, cols], op=ADD)
+            nc.sync.dma_start(out=out_rows[:, j, cols], in_=out_sb[:, j, cols])
 
-        spread_biases(0)
-        quantise_x(0)
-        spread_biases(1)
-        stage1(0)
-        quantise_x(1)
-        quantise_h(0)
+        sort_planes(0)
+        transpose_x(0)
         for e in range(E):
-            if e + 1 < E:
-                stage1(e + 1)
-            if e + 2 < E:
-                spread_biases(e + 2)
-            out_sb = w1_out_pool.tile([P, TOK_TILES, H], F32, tag="w1_or_out", align_bytes=64)
-            stage2(e, 0, out_sb)
-            if e + 2 < E:
-                quantise_x(e + 2)
-            if e + 1 < E:
-                quantise_h(e + 1)
-            stage2(e, 1, out_sb)
+            spread_b2(e)
+        quantise_x(0)
+        sort_w1(0, 0)
+        sort_w1(0, 1)
+        for e in range(-1, E):
+            now = e + 1
+            ahead = e + 2
+            for c in range(I_PASSES):
+                if now < E:
+                    stage1(now, c)
+                if c == 1 and ahead < E:
+                    transpose_x(ahead)
+                if now < E:
+                    if c > 0:
+                        quantise_h(now, c - 1)
+                    interleave_h(now, c)
+                if e >= 0:
+                    stage2(e, c % TOK_TILES, c // TOK_TILES)
+                if c == 3 and now < E:
+                    quantise_h(now, c)
+                if ahead < E:
+                    if c == 1:
+                        sort_w1(ahead, 0)
+                    if c == 2 and ahead == 1:
+                        sort_planes(1)
+                    if c == 2:
+                        quantise_x(ahead)
+                    if c == 3:
+                        sort_w1(ahead, 1)

@@ -152,8 +152,8 @@ def tile_fusedthorexpert_e_kernel(tc, x, w1_words, w1_scales, b1, w2_words, w2_s
         def sort_w1(e, chunk):
             w1_sorted = w1_sorted_pool.tile([P, H_PASSES, W1_CHUNK_COLS], I32, align_bytes=64)
             nc.vector.tensor_copy(
-                out=w1_sorted[:].rearrange("p g n -> p (g n)").rearrange("p (c t m) -> p c t m", t=PACK, m=P),
-                in_=w1_raw_tiles[(e, chunk)][:].rearrange("p g n -> p (g n)").rearrange("p (c m t) -> p c t m", t=PACK, m=P),
+                out=w1_sorted[:].rearrange("p g n -> p (g n)").rearrange("p (c t m) -> p c m t", t=PACK, m=P),
+                in_=w1_raw_tiles[(e, chunk)][:].rearrange("p g n -> p (g n)").rearrange("p (c m t) -> p c m t", t=PACK, m=P),
             )
             w1_sorted_tiles[(e, chunk)] = w1_sorted
 

@@ -27,7 +27,7 @@ W1_CHUNK_PASSES = I_PASSES // W1_CHUNKS
 PLANES = 4
 QUADRANTS = 4
 PSUM_BANKS = 8
-SCALAR_INTERLEAVES = (0, 2)
+SCALAR_INTERLEAVES = ()
 
 FLOPS = 2 * E * C * H * I * 2
 
@@ -41,11 +41,11 @@ def tile_fusedthorexpert_e_kernel(tc, x, w1_words, w1_scales, b1, w2_words, w2_s
         w1_out_pool = ctx.enter_context(tc.tile_pool(name="w1_out_pool", bufs=E * W1_CHUNKS))
         w1_sorted_pool = ctx.enter_context(tc.tile_pool(name="w1_sorted_pool", bufs=2 * W1_CHUNKS))
         w2_pool = ctx.enter_context(tc.tile_pool(name="w2_pool", bufs=E * OUT_TILES))
-        x_grouped_pool = ctx.enter_context(tc.tile_pool(name="x_grouped_pool", bufs=2))
+        x_grouped_pool = ctx.enter_context(tc.tile_pool(name="x_grouped_pool", bufs=1))
         x_mx_pool = ctx.enter_context(tc.tile_pool(name="x_mx_pool", bufs=2))
-        h_pool = ctx.enter_context(tc.tile_pool(name="h_pool", bufs=3))
+        h_pool = ctx.enter_context(tc.tile_pool(name="h_pool", bufs=4))
         h_grouped_pool = ctx.enter_context(tc.tile_pool(name="h_grouped_pool", bufs=3))
-        h_mx_pool = ctx.enter_context(tc.tile_pool(name="h_mx_pool", bufs=2))
+        h_mx_pool = ctx.enter_context(tc.tile_pool(name="h_mx_pool", bufs=3))
         psum = ctx.enter_context(tc.psum_pool(name="psum", bufs=PSUM_BANKS))
 
         w1_planes_raw = consts.tile([P, E * H_PASSES // PLANES, I], U8, align_bytes=64)
@@ -265,35 +265,59 @@ def tile_fusedthorexpert_e_kernel(tc, x, w1_words, w1_scales, b1, w2_words, w2_s
             nc.vector.tensor_tensor(out=out_sb[:, j, cols], in0=acc[:], in1=b2_all[:, e, cols], op=ADD)
             nc.sync.dma_start(out=out_rows[:, j, cols], in_=out_sb[:, j, cols])
 
+        def finish_h(e, chunk):
+            first = W1_CHUNK_PASSES * chunk
+            for c in range(first, first + W1_CHUNK_PASSES):
+                interleave_h(e, c)
+            for c in range(first, first + W1_CHUNK_PASSES):
+                quantise_h(e, c)
+
+        def stage1_chunk(e, chunk):
+            first = W1_CHUNK_PASSES * chunk
+            for c in range(first, first + W1_CHUNK_PASSES):
+                stage1(e, c)
+
+        def stage2_chunk(e, n):
+            for j in range(TOK_TILES):
+                stage2(e, j, n)
+
         sort_planes(0)
         transpose_x(0)
-        for e in range(E):
-            spread_b2(e)
+        spread_b2(0)
+        spread_b2(1)
         quantise_x(0)
         sort_w1(0, 0)
+        stage1_chunk(0, 0)
         sort_w1(0, 1)
-        for e in range(-1, E):
-            now = e + 1
+        transpose_x(1)
+        stage1_chunk(0, 1)
+        finish_h(0, 0)
+        quantise_x(1)
+        sort_w1(1, 0)
+        stage1_chunk(1, 0)
+        finish_h(0, 1)
+        sort_w1(1, 1)
+        transpose_x(2)
+        stage1_chunk(1, 1)
+        finish_h(1, 0)
+        quantise_x(2)
+        sort_planes(1)
+        spread_b2(2)
+        spread_b2(3)
+        finish_h(1, 1)
+        for e in range(E):
             ahead = e + 2
-            for c in range(I_PASSES):
-                if now < E:
-                    stage1(now, c)
-                if c == 1 and ahead < E:
-                    transpose_x(ahead)
-                if now < E:
-                    if c > 0:
-                        quantise_h(now, c - 1)
-                    interleave_h(now, c)
-                if e >= 0:
-                    stage2(e, c % TOK_TILES, c // TOK_TILES)
-                if c == 3 and now < E:
-                    quantise_h(now, c)
+            for half in range(2):
                 if ahead < E:
-                    if c == 1:
-                        sort_w1(ahead, 0)
-                    if c == 2 and ahead == 1:
-                        sort_planes(1)
-                    if c == 2:
-                        quantise_x(ahead)
-                    if c == 3:
-                        sort_w1(ahead, 1)
+                    sort_w1(ahead, half)
+                stage2_chunk(e, half)
+                if ahead < E:
+                    if half == 1:
+                        finish_h(ahead, 0)
+                    if half == 1 and ahead + 1 < E:
+                        transpose_x(ahead + 1)
+                    stage1_chunk(ahead, half)
+            if ahead + 1 < E:
+                quantise_x(ahead + 1)
+            if ahead < E:
+                finish_h(ahead, 1)

@@ -40,7 +40,7 @@ def tile_fusedthorexpert_e_kernel(tc, x, w1_words, w1_scales, b1, w2_words, w2_s
         x_pool = ctx.enter_context(tc.tile_pool(name="x_pool", bufs=3))
         w1_out_pool = ctx.enter_context(tc.tile_pool(name="w1_out_pool", bufs=E * W1_CHUNKS))
         w1_sorted_pool = ctx.enter_context(tc.tile_pool(name="w1_sorted_pool", bufs=2 * W1_CHUNKS))
-        w2_pool = ctx.enter_context(tc.tile_pool(name="w2_pool", bufs=E * OUT_TILES))
+        w2_pool = ctx.enter_context(tc.tile_pool(name="w2_pool", bufs=E))
         x_grouped_pool = ctx.enter_context(tc.tile_pool(name="x_grouped_pool", bufs=1))
         x_mx_pool = ctx.enter_context(tc.tile_pool(name="x_mx_pool", bufs=2))
         h_pool = ctx.enter_context(tc.tile_pool(name="h_pool", bufs=4))
@@ -94,11 +94,20 @@ def tile_fusedthorexpert_e_kernel(tc, x, w1_words, w1_scales, b1, w2_words, w2_s
             )
             w1_raw_tiles[(e, chunk)] = w1_raw
 
-        def load_w2(e, n):
+        def load_w2(e):
             words = w2_words[I_PASSES * e : I_PASSES * (e + 1)].rearrange("g p n t -> p g (n t)")
-            w2_sb = w2_pool.tile([P, I_PASSES, N_TILE], I32, align_bytes=64)
-            nc.sync.dma_start(out=w2_sb[:], in_=words[:, :, PACK * N_TILE * n : PACK * N_TILE * (n + 1)].bitcast(I32))
-            w2_tiles[(e, n)] = w2_sb
+            if e < E - 1:
+                w2_sb = w2_pool.tile([P, I_PASSES, H], I32, tag="w2", align_bytes=64)
+                nc.sync.dma_start(out=w2_sb[:], in_=words.bitcast(I32))
+                for n in range(OUT_TILES):
+                    for c in range(I_PASSES):
+                        w2_tiles[(e, c, n)] = w2_sb[:, c, N_TILE * n : N_TILE * (n + 1)]
+            else:
+                w2_halves = w2_pool.tile([P, OUT_TILES, I_PASSES, N_TILE], I32, tag="w2", align_bytes=64)
+                for n in range(OUT_TILES):
+                    nc.sync.dma_start(out=w2_halves[:, n], in_=words[:, :, PACK * N_TILE * n : PACK * N_TILE * (n + 1)].bitcast(I32))
+                    for c in range(I_PASSES):
+                        w2_tiles[(e, c, n)] = w2_halves[:, n, c, :]
 
         load_x(0)
         for a in range(E * H_PASSES // PLANES):
@@ -112,10 +121,10 @@ def tile_fusedthorexpert_e_kernel(tc, x, w1_words, w1_scales, b1, w2_words, w2_s
         for e in range(E):
             load_planes(w2_planes[:, e, :], w2_scales[PLANES * e : PLANES * (e + 1)])
         for e in range(E):
-            for half in range(2):
-                load_w2(e, half)
-                if e + 2 < E:
-                    load_w1(e + 2, half)
+            load_w2(e)
+            if e + 2 < E:
+                load_w1(e + 2, 0)
+                load_w1(e + 2, 1)
             if e + 3 < E:
                 load_x(e + 3)
 
@@ -257,13 +266,16 @@ def tile_fusedthorexpert_e_kernel(tc, x, w1_words, w1_scales, b1, w2_words, w2_s
                     out=acc[:],
                     lhsT=h_codes[:, tokens].bitcast(FP8X4),
                     lhsT_scale=h_scales[:, tokens],
-                    rhs=w2_tiles[(e, n)][:, c, :].bitcast(FP8X4),
+                    rhs=w2_tiles[(e, c, n)].bitcast(FP8X4),
                     rhs_scale=w2_planes[4 * c : P, e, cols],
                     start=(c == 0),
                     stop=(c == I_PASSES - 1),
                 )
             nc.vector.tensor_tensor(out=out_sb[:, j, cols], in0=acc[:], in1=b2_all[:, e, cols], op=ADD)
-            nc.sync.dma_start(out=out_rows[:, j, cols], in_=out_sb[:, j, cols])
+            if e == E - 1:
+                nc.sync.dma_start(out=out_rows[:, j, cols], in_=out_sb[:, j, cols])
+            elif n == OUT_TILES - 1:
+                nc.sync.dma_start(out=out_rows[:, j, :], in_=out_sb[:, j, :])
 
         def finish_h(e, chunk):
             first = W1_CHUNK_PASSES * chunk
@@ -277,9 +289,12 @@ def tile_fusedthorexpert_e_kernel(tc, x, w1_words, w1_scales, b1, w2_words, w2_s
             for c in range(first, first + W1_CHUNK_PASSES):
                 stage1(e, c)
 
-        def stage2_chunk(e, n):
-            for j in range(TOK_TILES):
-                stage2(e, j, n)
+        def stage2_chunk(e, half):
+            for other in range(2):
+                if e == E - 1:
+                    stage2(e, other, half)
+                else:
+                    stage2(e, half, other)
 
         sort_planes(0)
         transpose_x(0)
@@ -307,17 +322,17 @@ def tile_fusedthorexpert_e_kernel(tc, x, w1_words, w1_scales, b1, w2_words, w2_s
         finish_h(1, 1)
         for e in range(E):
             ahead = e + 2
-            for half in range(2):
-                if ahead < E:
-                    sort_w1(ahead, half)
-                stage2_chunk(e, half)
-                if ahead < E:
-                    if half == 1:
-                        finish_h(ahead, 0)
-                    if half == 1 and ahead + 1 < E:
-                        transpose_x(ahead + 1)
-                    stage1_chunk(ahead, half)
-            if ahead + 1 < E:
-                quantise_x(ahead + 1)
+            stage2_chunk(e, 0)
             if ahead < E:
+                sort_w1(ahead, 0)
+            stage2_chunk(e, 1)
+            if ahead < E:
+                sort_w1(ahead, 1)
+                stage1_chunk(ahead, 0)
+                stage1_chunk(ahead, 1)
+                finish_h(ahead, 0)
+                if ahead + 1 < E:
+                    transpose_x(ahead + 1)
                 finish_h(ahead, 1)
+                if ahead + 1 < E:
+                    quantise_x(ahead + 1)

@@ -159,10 +159,10 @@ def tile_fusedthorexpert_e_kernel(tc, x, w1_words, w1_scales, b1, w2_words, w2_s
         w1_sorted_tiles = {}
 
         def sort_w1(e, chunk):
-            w1_sorted = w1_sorted_pool.tile([P, H_PASSES, W1_CHUNK_COLS], I32, align_bytes=64)
+            w1_sorted = w1_sorted_pool.tile([P, PACK, H_PASSES * W1_CHUNK_PASSES, P], I32, align_bytes=64)
             nc.vector.tensor_copy(
-                out=w1_sorted[:].rearrange("p g n -> p (g n)").rearrange("p (c t m) -> p c m t", t=PACK, m=P),
-                in_=w1_raw_tiles[(e, chunk)][:].rearrange("p g n -> p (g n)").rearrange("p (c m t) -> p c m t", t=PACK, m=P),
+                out=w1_sorted[:].rearrange("p t b m -> p (t b m)").rearrange("p (t q i) -> p q t i", t=PACK, i=4),
+                in_=w1_raw_tiles[(e, chunk)][:].rearrange("p g n -> p (g n)").rearrange("p (q i t) -> p q t i", t=PACK, i=4),
             )
             w1_sorted_tiles[(e, chunk)] = w1_sorted
 
@@ -204,12 +204,11 @@ def tile_fusedthorexpert_e_kernel(tc, x, w1_words, w1_scales, b1, w2_words, w2_s
                 bank = psum.tile([P, 2, C], F32, tag="bank")
                 for s in range(2):
                     t = 2 * half + s
-                    first = K_PASS * (c % W1_CHUNK_PASSES) + P * t
                     for g in range(H_PASSES):
                         a, i = divmod(H_PASSES * e + g, PLANES)
                         nc.tensor.matmul_mx(
                             out=bank[:, s, :],
-                            lhsT=w1_sorted[:, g, first : first + P].bitcast(FP8X4),
+                            lhsT=w1_sorted[:, t, W1_CHUNK_PASSES * g + c % W1_CHUNK_PASSES, :].bitcast(FP8X4),
                             lhsT_scale=w1_planes[4 * i : P, a, K_PASS * c + P * t : K_PASS * c + P * (t + 1)],
                             rhs=x_codes[:, C * g : C * (g + 1)].bitcast(FP8X4),
                             rhs_scale=x_scales[:, C * g : C * (g + 1)],

@@ -69,12 +69,13 @@ def tile_fusedthorexpert_e_kernel(tc, x, w1_words, w1_scales, b1, w2_words, w2_s
         ident_f32 = consts.tile([P, P], F32)
         make_identity(nc, ident_f32[:])
 
-        def load_planes(planes, scales):
+        def load_planes(planes, scales, early):
             for quadrant in range(QUADRANTS):
-                nc.sync.dma_start(
-                    out=planes[32 * quadrant : 32 * quadrant + 4 * PLANES, :].bitcast(I32),
-                    in_=scales[:, 4 * quadrant : 4 * quadrant + 4, :].bitcast(I32),
-                )
+                rows = slice(32 * quadrant, 32 * quadrant + 4 * PLANES)
+                if early:
+                    nc.sync.dma_start(out=planes[rows, :].bitcast(I32), in_=scales[:, 4 * quadrant : 4 * quadrant + 4, :].bitcast(I32))
+                else:
+                    nc.gpsimd.dma_start(out=planes[rows, :].bitcast(F32), in_=scales[:, 4 * quadrant : 4 * quadrant + 4, :].bitcast(F32))
 
         x_tiles = {}
         w1_raw_tiles = {}
@@ -110,16 +111,16 @@ def tile_fusedthorexpert_e_kernel(tc, x, w1_words, w1_scales, b1, w2_words, w2_s
                         w2_tiles[(e, c, n)] = w2_halves[:, n, c, :]
 
         load_x(0)
-        for a in range(E * H_PASSES // PLANES):
-            load_planes(w1_planes_raw[:, a, :], w1_scales[PLANES * a : PLANES * (a + 1)])
+        load_planes(w1_planes_raw[:, 0, :], w1_scales[0:PLANES], True)
+        load_planes(w1_planes_raw[:, 1, :], w1_scales[PLANES : 2 * PLANES], False)
+        for e in range(E):
+            load_planes(w2_planes[:, e, :], w2_scales[PLANES * e : PLANES * (e + 1)], False)
         load_w1(0, 0)
         load_w1(0, 1)
         load_x(1)
         load_w1(1, 0)
         load_w1(1, 1)
         load_x(2)
-        for e in range(E):
-            load_planes(w2_planes[:, e, :], w2_scales[PLANES * e : PLANES * (e + 1)])
         for e in range(E):
             load_w2(e)
             if e + 2 < E:

@@ -111,9 +111,9 @@ def tile_fusedthorexpert_e_kernel(tc, x, w1_words, w1_scales, b1, w2_words, w2_s
                         w2_tiles[(e, c, n)] = w2_halves[:, n, c, :]
 
         load_x(0)
-        load_planes(w1_planes_raw[:, 0, :], w1_scales[0:PLANES], True)
-        load_planes(w1_planes_raw[:, 1, :], w1_scales[PLANES : 2 * PLANES], False)
-        for e in range(E):
+        for a in range(E * H_PASSES // PLANES):
+            load_planes(w1_planes_raw[:, a, :], w1_scales[PLANES * a : PLANES * (a + 1)], True)
+        for e in range(1, E):
             load_planes(w2_planes[:, e, :], w2_scales[PLANES * e : PLANES * (e + 1)], False)
         load_w1(0, 0)
         load_w1(0, 1)
@@ -121,6 +121,7 @@ def tile_fusedthorexpert_e_kernel(tc, x, w1_words, w1_scales, b1, w2_words, w2_s
         load_w1(1, 0)
         load_w1(1, 1)
         load_x(2)
+        load_planes(w2_planes[:, 0, :], w2_scales[0:PLANES], True)
         for e in range(E):
             load_w2(e)
             if e + 2 < E:

@@ -21,9 +21,9 @@ TOK_TILES = C // P
 H_PASSES = H // K_PASS
 I_PASSES = I // K_PASS
 OUT_TILES = H // N_TILE
-W1_CHUNKS = 2
-W1_CHUNK_COLS = I // W1_CHUNKS
-W1_CHUNK_PASSES = I_PASSES // W1_CHUNKS
+W1_CHUNKS_FIRST = ((0, 1), (1, 1), (2, 2))
+W1_CHUNKS_LATER = ((0, 2), (2, 2))
+W1_SLOTS = 8
 PLANES = 4
 QUADRANTS = 4
 PSUM_BANKS = 8
@@ -38,8 +38,8 @@ def tile_fusedthorexpert_e_kernel(tc, x, w1_words, w1_scales, b1, w2_words, w2_s
         ctx.enter_context(tc.manual_schedule())
         consts = ctx.enter_context(tc.tile_pool(name="consts", bufs=1))
         x_pool = ctx.enter_context(tc.tile_pool(name="x_pool", bufs=3))
-        w1_out_pool = ctx.enter_context(tc.tile_pool(name="w1_out_pool", bufs=E * W1_CHUNKS))
-        w1_sorted_pool = ctx.enter_context(tc.tile_pool(name="w1_sorted_pool", bufs=2 * W1_CHUNKS))
+        w1_out_pool = ctx.enter_context(tc.tile_pool(name="w1_out_pool", bufs=W1_SLOTS))
+        w1_sorted_pool = ctx.enter_context(tc.tile_pool(name="w1_sorted_pool", bufs=4))
         w2_pool = ctx.enter_context(tc.tile_pool(name="w2_pool", bufs=E))
         x_grouped_pool = ctx.enter_context(tc.tile_pool(name="x_grouped_pool", bufs=1))
         x_mx_pool = ctx.enter_context(tc.tile_pool(name="x_mx_pool", bufs=2))
@@ -47,6 +47,11 @@ def tile_fusedthorexpert_e_kernel(tc, x, w1_words, w1_scales, b1, w2_words, w2_s
         h_grouped_pool = ctx.enter_context(tc.tile_pool(name="h_grouped_pool", bufs=3))
         h_mx_pool = ctx.enter_context(tc.tile_pool(name="h_mx_pool", bufs=3))
         psum = ctx.enter_context(tc.psum_pool(name="psum", bufs=PSUM_BANKS))
+
+        warm_in = consts.tile([P, 1], F32)
+        warm_out = consts.tile([P, 1], F32)
+        nc.vector.memset(warm_in[:], 0.0)
+        nc.scalar.activation(out=warm_out[:], in_=warm_in[:], func=GELU)
 
         w1_planes_raw = consts.tile([P, E * H_PASSES // PLANES, I], U8, align_bytes=64)
         w1_planes = consts.tile([P, E * H_PASSES // PLANES, I], U8, align_bytes=64)
@@ -57,17 +62,12 @@ def tile_fusedthorexpert_e_kernel(tc, x, w1_words, w1_scales, b1, w2_words, w2_s
         nc.vector.memset(bias_rows[:].bitcast(I32), 0)
         nc.scalar.dma_start(out=bias_rows[0 : E * I_PASSES, 0:K_PASS], in_=b1.rearrange("e (c k) -> (e c) k", k=K_PASS))
         nc.scalar.dma_start(out=bias_rows[0:E, K_PASS : K_PASS + H], in_=b2)
-        nc.vector.memset(w2_planes[:].rearrange("p a n -> p (a n)").bitcast(I32), 0)
 
-        warm_in = consts.tile([P, 1], F32)
-        warm_out = consts.tile([P, 1], F32)
-        nc.vector.memset(warm_in[:], 0.0)
-        nc.scalar.activation(out=warm_out[:], in_=warm_in[:], func=GELU)
-
-        ident_bf16 = consts.tile([P, P], BF16)
-        make_identity(nc, ident_bf16[:])
         ident_f32 = consts.tile([P, P], F32)
         make_identity(nc, ident_f32[:])
+        ident_bf16 = consts.tile([P, P], BF16)
+        make_identity(nc, ident_bf16[:])
+        nc.gpsimd.memset(w2_planes[:].rearrange("p a n -> p (a n)").bitcast(F32), 0.0)
 
         def load_planes(planes, scales, early):
             for quadrant in range(QUADRANTS):
@@ -86,12 +86,16 @@ def tile_fusedthorexpert_e_kernel(tc, x, w1_words, w1_scales, b1, w2_words, w2_s
             nc.sync.dma_start(out=x_sb[:], in_=x[C * e : C * (e + 1), :].rearrange("(p j) k -> p j k", j=TOK_TILES))
             x_tiles[e] = x_sb
 
+        def w1_chunks(e):
+            return W1_CHUNKS_FIRST if e == 0 else W1_CHUNKS_LATER
+
         def load_w1(e, chunk):
+            first, passes = w1_chunks(e)[chunk]
             words = w1_words[H_PASSES * e : H_PASSES * (e + 1)].rearrange("g p n t -> p g (n t)")
-            w1_raw = w1_out_pool.tile([P, H_PASSES, W1_CHUNK_COLS], I32, tag="w1_or_out", align_bytes=64)
+            w1_raw = w1_out_pool.tile([P, H_PASSES, K_PASS * passes], I32, tag="w1_or_out", align_bytes=64)
             nc.sync.dma_start(
                 out=w1_raw[:],
-                in_=words[:, :, PACK * W1_CHUNK_COLS * chunk : PACK * W1_CHUNK_COLS * (chunk + 1)].bitcast(I32),
+                in_=words[:, :, PACK * K_PASS * first : PACK * K_PASS * (first + passes)].bitcast(I32),
             )
             w1_raw_tiles[(e, chunk)] = w1_raw
 
@@ -111,16 +115,16 @@ def tile_fusedthorexpert_e_kernel(tc, x, w1_words, w1_scales, b1, w2_words, w2_s
                         w2_tiles[(e, c, n)] = w2_halves[:, n, c, :]
 
         load_x(0)
-        for a in range(E * H_PASSES // PLANES):
-            load_planes(w1_planes_raw[:, a, :], w1_scales[PLANES * a : PLANES * (a + 1)], True)
+        load_planes(w1_planes_raw[:, 0, :], w1_scales[0:PLANES], True)
         for e in range(1, E):
             load_planes(w2_planes[:, e, :], w2_scales[PLANES * e : PLANES * (e + 1)], False)
-        load_w1(0, 0)
-        load_w1(0, 1)
+        for chunk in range(len(w1_chunks(0))):
+            load_w1(0, chunk)
         load_x(1)
         load_w1(1, 0)
         load_w1(1, 1)
         load_x(2)
+        load_planes(w1_planes_raw[:, 1, :], w1_scales[PLANES : 2 * PLANES], True)
         load_planes(w2_planes[:, 0, :], w2_scales[0:PLANES], True)
         for e in range(E):
             load_w2(e)
@@ -130,11 +134,13 @@ def tile_fusedthorexpert_e_kernel(tc, x, w1_words, w1_scales, b1, w2_words, w2_s
             if e + 3 < E:
                 load_x(e + 3)
 
-        b1_bank = psum.tile([P, PACK, P], BF16, tag="bank")
-        for t in range(PACK):
-            nc.tensor.transpose(b1_bank[:, t, :], bias_rows[:, t:K_PASS:PACK], ident_bf16[:])
         b1_cols = consts.tile([P, PACK, E * I_PASSES], F32)
-        nc.vector.tensor_copy(out=b1_cols[:], in_=b1_bank[:, :, 0 : E * I_PASSES])
+
+        def turn_b1():
+            b1_bank = psum.tile([P, PACK, P], BF16, tag="bank")
+            for t in range(PACK):
+                nc.tensor.transpose(b1_bank[:, t, :], bias_rows[:, t:K_PASS:PACK], ident_bf16[:])
+            nc.vector.tensor_copy(out=b1_cols[:], in_=b1_bank[:, :, 0 : E * I_PASSES])
 
         b2_all = consts.tile([P, E, H], BF16)
 
@@ -151,22 +157,27 @@ def tile_fusedthorexpert_e_kernel(tc, x, w1_words, w1_scales, b1, w2_words, w2_s
                 )
             nc.scalar.copy(out=b2_all[:, e, :], in_=bank[:])
 
-        def sort_planes(a):
+        def sort_planes(a, half):
+            cols = slice(I // 2 * half, I // 2 * (half + 1))
             for t in range(PACK):
                 nc.vector.tensor_copy(
-                    out=w1_planes[:, a, :].rearrange("p (c t m) -> p t c m", t=PACK, m=P)[:, t],
-                    in_=w1_planes_raw[:, a, :].rearrange("p (c m t) -> p t c m", t=PACK, m=P)[:, t],
+                    out=w1_planes[:, a, cols].rearrange("p (c t m) -> p t c m", t=PACK, m=P)[:, t],
+                    in_=w1_planes_raw[:, a, cols].rearrange("p (c m t) -> p t c m", t=PACK, m=P)[:, t],
                 )
 
         w1_sorted_tiles = {}
 
         def sort_w1(e, chunk):
-            w1_sorted = w1_sorted_pool.tile([P, PACK, H_PASSES * W1_CHUNK_PASSES, P], I32, align_bytes=64)
+            first, passes = w1_chunks(e)[chunk]
+            w1_sorted = w1_sorted_pool.tile([P, PACK, H_PASSES * passes, P], I32, align_bytes=64)
             nc.vector.tensor_copy(
                 out=w1_sorted[:].rearrange("p t b m -> p (t b m)").rearrange("p (t q i) -> p q t i", t=PACK, i=4),
                 in_=w1_raw_tiles[(e, chunk)][:].rearrange("p g n -> p (g n)").rearrange("p (q i t) -> p q t i", t=PACK, i=4),
             )
-            w1_sorted_tiles[(e, chunk)] = w1_sorted
+            for c in range(first, first + passes):
+                for g in range(H_PASSES):
+                    for t in range(PACK):
+                        w1_sorted_tiles[(e, c, g, t)] = w1_sorted[:, t, passes * g + c - first, :]
 
         x_grouped_tiles = {}
         x_mx = {}
@@ -200,7 +211,6 @@ def tile_fusedthorexpert_e_kernel(tc, x, w1_words, w1_scales, b1, w2_words, w2_s
 
         def stage1(e, c):
             x_codes, x_scales = x_mx[e]
-            w1_sorted = w1_sorted_tiles[(e, c // W1_CHUNK_PASSES)]
             h_rows = h_pool.tile([P, PACK, C], BF16)
             for half in range(2):
                 bank = psum.tile([P, 2, C], F32, tag="bank")
@@ -210,7 +220,7 @@ def tile_fusedthorexpert_e_kernel(tc, x, w1_words, w1_scales, b1, w2_words, w2_s
                         a, i = divmod(H_PASSES * e + g, PLANES)
                         nc.tensor.matmul_mx(
                             out=bank[:, s, :],
-                            lhsT=w1_sorted[:, t, W1_CHUNK_PASSES * g + c % W1_CHUNK_PASSES, :].bitcast(FP8X4),
+                            lhsT=w1_sorted_tiles[(e, c, g, t)].bitcast(FP8X4),
                             lhsT_scale=w1_planes[4 * i : P, a, K_PASS * c + P * t : K_PASS * c + P * (t + 1)],
                             rhs=x_codes[:, C * g : C * (g + 1)].bitcast(FP8X4),
                             rhs_scale=x_scales[:, C * g : C * (g + 1)],
@@ -278,16 +288,15 @@ def tile_fusedthorexpert_e_kernel(tc, x, w1_words, w1_scales, b1, w2_words, w2_s
             elif n == OUT_TILES - 1:
                 nc.sync.dma_start(out=out_rows[:, j, :], in_=out_sb[:, j, :])
 
-        def finish_h(e, chunk):
-            first = W1_CHUNK_PASSES * chunk
-            for c in range(first, first + W1_CHUNK_PASSES):
+        def finish_h(e, half):
+            for c in (2 * half, 2 * half + 1):
                 interleave_h(e, c)
-            for c in range(first, first + W1_CHUNK_PASSES):
+            for c in (2 * half, 2 * half + 1):
                 quantise_h(e, c)
 
         def stage1_chunk(e, chunk):
-            first = W1_CHUNK_PASSES * chunk
-            for c in range(first, first + W1_CHUNK_PASSES):
+            first, passes = w1_chunks(e)[chunk]
+            for c in range(first, first + passes):
                 stage1(e, c)
 
         def stage2_chunk(e, half):
@@ -297,16 +306,20 @@ def tile_fusedthorexpert_e_kernel(tc, x, w1_words, w1_scales, b1, w2_words, w2_s
                 else:
                     stage2(e, half, other)
 
-        sort_planes(0)
         transpose_x(0)
+        turn_b1()
         spread_b2(0)
         spread_b2(1)
+        sort_planes(0, 0)
         quantise_x(0)
         sort_w1(0, 0)
         stage1_chunk(0, 0)
         sort_w1(0, 1)
-        transpose_x(1)
         stage1_chunk(0, 1)
+        sort_planes(0, 1)
+        sort_w1(0, 2)
+        transpose_x(1)
+        stage1_chunk(0, 2)
         finish_h(0, 0)
         quantise_x(1)
         sort_w1(1, 0)
@@ -317,7 +330,8 @@ def tile_fusedthorexpert_e_kernel(tc, x, w1_words, w1_scales, b1, w2_words, w2_s
         stage1_chunk(1, 1)
         finish_h(1, 0)
         quantise_x(2)
-        sort_planes(1)
+        sort_planes(1, 0)
+        sort_planes(1, 1)
         spread_b2(2)
         spread_b2(3)
         finish_h(1, 1)

@@ -62,12 +62,12 @@ def tile_fusedthorexpert_e_kernel(tc, x, w1_words, w1_scales, b1, w2_words, w2_s
         nc.vector.memset(bias_rows[:].bitcast(I32), 0)
         nc.scalar.dma_start(out=bias_rows[0 : E * I_PASSES, 0:K_PASS], in_=b1.rearrange("e (c k) -> (e c) k", k=K_PASS))
         nc.scalar.dma_start(out=bias_rows[0:E, K_PASS : K_PASS + H], in_=b2)
+        nc.vector.memset(w2_planes[:].rearrange("p a n -> p (a n)").bitcast(I32), 0)
 
         ident_f32 = consts.tile([P, P], F32)
         make_identity(nc, ident_f32[:])
         ident_bf16 = consts.tile([P, P], BF16)
         make_identity(nc, ident_bf16[:])
-        nc.gpsimd.memset(w2_planes[:].rearrange("p a n -> p (a n)").bitcast(F32), 0.0)
 
         def load_planes(planes, scales, early):
             for quadrant in range(QUADRANTS):
@@ -115,7 +115,8 @@ def tile_fusedthorexpert_e_kernel(tc, x, w1_words, w1_scales, b1, w2_words, w2_s
                         w2_tiles[(e, c, n)] = w2_halves[:, n, c, :]
 
         load_x(0)
-        load_planes(w1_planes_raw[:, 0, :], w1_scales[0:PLANES], True)
+        for a in range(E * H_PASSES // PLANES):
+            load_planes(w1_planes_raw[:, a, :], w1_scales[PLANES * a : PLANES * (a + 1)], True)
         for e in range(1, E):
             load_planes(w2_planes[:, e, :], w2_scales[PLANES * e : PLANES * (e + 1)], False)
         for chunk in range(len(w1_chunks(0))):
@@ -124,7 +125,6 @@ def tile_fusedthorexpert_e_kernel(tc, x, w1_words, w1_scales, b1, w2_words, w2_s
         load_w1(1, 0)
         load_w1(1, 1)
         load_x(2)
-        load_planes(w1_planes_raw[:, 1, :], w1_scales[PLANES : 2 * PLANES], True)
         load_planes(w2_planes[:, 0, :], w2_scales[0:PLANES], True)
         for e in range(E):
             load_w2(e)

from contextlib import ExitStack

import concourse.mybir as mybir
from concourse.masks import make_identity

BF16 = mybir.dt.bfloat16
F32 = mybir.dt.float32
I32 = mybir.dt.int32
U32 = mybir.dt.uint32
U8 = mybir.dt.uint8
FP8X4 = mybir.dt.float8_e4m3fn_x4
ADD = mybir.AluOpType.add
GELU = mybir.ActivationFunctionType.Gelu

E, C, H, I = 4, 256, 1024, 2048
P = 128
PACK = 4
K_PASS = P * PACK
N_TILE = 512
TOK_TILES = C // P
H_PASSES = H // K_PASS
I_PASSES = I // K_PASS
OUT_TILES = H // N_TILE
W1_CHUNKS_FIRST = ((0, 1), (1, 1), (2, 2))
W1_CHUNKS_LATER = ((0, 2), (2, 2))
W1_SLOTS = 8
PLANES = 4
QUADRANTS = 4
PSUM_BANKS = 8
SCALAR_INTERLEAVES = ()

FLOPS = 2 * E * C * H * I * 2


def tile_fusedthorexpert_e_kernel(tc, x, w1_words, w1_scales, b1, w2_words, w2_scales, b2, out):
    nc = tc.nc
    with ExitStack() as ctx:
        ctx.enter_context(tc.manual_schedule())
        consts = ctx.enter_context(tc.tile_pool(name="consts", bufs=1))
        x_pool = ctx.enter_context(tc.tile_pool(name="x_pool", bufs=3))
        w1_out_pool = ctx.enter_context(tc.tile_pool(name="w1_out_pool", bufs=W1_SLOTS))
        w1_sorted_pool = ctx.enter_context(tc.tile_pool(name="w1_sorted_pool", bufs=4))
        w2_pool = ctx.enter_context(tc.tile_pool(name="w2_pool", bufs=E))
        x_grouped_pool = ctx.enter_context(tc.tile_pool(name="x_grouped_pool", bufs=1))
        x_mx_pool = ctx.enter_context(tc.tile_pool(name="x_mx_pool", bufs=2))
        h_pool = ctx.enter_context(tc.tile_pool(name="h_pool", bufs=4))
        h_grouped_pool = ctx.enter_context(tc.tile_pool(name="h_grouped_pool", bufs=3))
        h_mx_pool = ctx.enter_context(tc.tile_pool(name="h_mx_pool", bufs=3))
        psum = ctx.enter_context(tc.psum_pool(name="psum", bufs=PSUM_BANKS))

        warm_in = consts.tile([P, 1], F32)
        warm_out = consts.tile([P, 1], F32)
        nc.vector.memset(warm_in[:], 0.0)
        nc.scalar.activation(out=warm_out[:], in_=warm_in[:], func=GELU)

        w1_planes_raw = consts.tile([P, E * H_PASSES // PLANES, I], U8, align_bytes=64)
        w1_planes = consts.tile([P, E * H_PASSES // PLANES, I], U8, align_bytes=64)
        w2_planes = consts.tile([P, E * I_PASSES // PLANES, H], U8, align_bytes=64)
        nc.vector.memset(w1_planes_raw[:].rearrange("p a n -> p (a n)").bitcast(I32), 0)

        bias_rows = consts.tile([P, K_PASS + H], BF16)
        nc.vector.memset(bias_rows[:].bitcast(I32), 0)
        nc.scalar.dma_start(out=bias_rows[0 : E * I_PASSES, 0:K_PASS], in_=b1.rearrange("e (c k) -> (e c) k", k=K_PASS))
        nc.scalar.dma_start(out=bias_rows[0:E, K_PASS : K_PASS + H], in_=b2)
        nc.vector.memset(w2_planes[:].rearrange("p a n -> p (a n)").bitcast(I32), 0)

        ident_f32 = consts.tile([P, P], F32)
        make_identity(nc, ident_f32[:])
        ident_bf16 = consts.tile([P, P], BF16)
        make_identity(nc, ident_bf16[:])

        def load_planes(planes, scales, early):
            for quadrant in range(QUADRANTS):
                rows = slice(32 * quadrant, 32 * quadrant + 4 * PLANES)
                if early:
                    nc.sync.dma_start(out=planes[rows, :].bitcast(I32), in_=scales[:, 4 * quadrant : 4 * quadrant + 4, :].bitcast(I32))
                else:
                    nc.gpsimd.dma_start(out=planes[rows, :].bitcast(F32), in_=scales[:, 4 * quadrant : 4 * quadrant + 4, :].bitcast(F32))

        x_tiles = {}
        w1_raw_tiles = {}
        w2_tiles = {}

        def load_x(e):
            x_sb = x_pool.tile([P, TOK_TILES, H], BF16)
            nc.sync.dma_start(out=x_sb[:], in_=x[C * e : C * (e + 1), :].rearrange("(p j) k -> p j k", j=TOK_TILES))
            x_tiles[e] = x_sb

        def w1_chunks(e):
            return W1_CHUNKS_FIRST if e == 0 else W1_CHUNKS_LATER

        def load_w1(e, chunk):
            first, passes = w1_chunks(e)[chunk]
            words = w1_words[H_PASSES * e : H_PASSES * (e + 1)].rearrange("g p n t -> p g (n t)")
            w1_raw = w1_out_pool.tile([P, H_PASSES, K_PASS * passes], I32, tag="w1_or_out", align_bytes=64)
            nc.sync.dma_start(
                out=w1_raw[:],
                in_=words[:, :, PACK * K_PASS * first : PACK * K_PASS * (first + passes)].bitcast(I32),
            )
            w1_raw_tiles[(e, chunk)] = w1_raw

        def load_w2(e):
            words = w2_words[I_PASSES * e : I_PASSES * (e + 1)].rearrange("g p n t -> p g (n t)")
            if e < E - 1:
                w2_sb = w2_pool.tile([P, I_PASSES, H], I32, tag="w2", align_bytes=64)
                nc.sync.dma_start(out=w2_sb[:], in_=words.bitcast(I32))
                for n in range(OUT_TILES):
                    for c in range(I_PASSES):
                        w2_tiles[(e, c, n)] = w2_sb[:, c, N_TILE * n : N_TILE * (n + 1)]
            else:
                w2_halves = w2_pool.tile([P, OUT_TILES, I_PASSES, N_TILE], I32, tag="w2", align_bytes=64)
                for n in range(OUT_TILES):
                    nc.sync.dma_start(out=w2_halves[:, n], in_=words[:, :, PACK * N_TILE * n : PACK * N_TILE * (n + 1)].bitcast(I32))
                    for c in range(I_PASSES):
                        w2_tiles[(e, c, n)] = w2_halves[:, n, c, :]

        load_x(0)
        for a in range(E * H_PASSES // PLANES):
            load_planes(w1_planes_raw[:, a, :], w1_scales[PLANES * a : PLANES * (a + 1)], True)
        for e in range(1, E):
            load_planes(w2_planes[:, e, :], w2_scales[PLANES * e : PLANES * (e + 1)], False)
        for chunk in range(len(w1_chunks(0))):
            load_w1(0, chunk)
        load_x(1)
        load_w1(1, 0)
        load_w1(1, 1)
        load_x(2)
        load_planes(w2_planes[:, 0, :], w2_scales[0:PLANES], True)
        for e in range(E):
            load_w2(e)
            if e + 2 < E:
                load_w1(e + 2, 0)
                load_w1(e + 2, 1)
            if e + 3 < E:
                load_x(e + 3)

        b1_cols = consts.tile([P, PACK, E * I_PASSES], F32)

        def turn_b1():
            b1_bank = psum.tile([P, PACK, P], BF16, tag="bank")
            for t in range(PACK):
                nc.tensor.transpose(b1_bank[:, t, :], bias_rows[:, t:K_PASS:PACK], ident_bf16[:])
            nc.vector.tensor_copy(out=b1_cols[:], in_=b1_bank[:, :, 0 : E * I_PASSES])

        b2_all = consts.tile([P, E, H], BF16)

        def spread_b2(e):
            pick_row = ident_bf16[:, e : e + 1].to_broadcast([P, P])
            bank = psum.tile([P, H], BF16, tag="bank")
            for n in range(OUT_TILES):
                nc.tensor.matmul(
                    out=bank[:, N_TILE * n : N_TILE * (n + 1)],
                    lhsT=pick_row,
                    rhs=bias_rows[:, K_PASS + N_TILE * n : K_PASS + N_TILE * (n + 1)],
                    start=True,
                    stop=True,
                )
            nc.scalar.copy(out=b2_all[:, e, :], in_=bank[:])

        def sort_planes(a, half):
            cols = slice(I // 2 * half, I // 2 * (half + 1))
            for t in range(PACK):
                nc.vector.tensor_copy(
                    out=w1_planes[:, a, cols].rearrange("p (c t m) -> p t c m", t=PACK, m=P)[:, t],
                    in_=w1_planes_raw[:, a, cols].rearrange("p (c m t) -> p t c m", t=PACK, m=P)[:, t],
                )

        w1_sorted_tiles = {}

        def sort_w1(e, chunk):
            first, passes = w1_chunks(e)[chunk]
            w1_sorted = w1_sorted_pool.tile([P, PACK, H_PASSES * passes, P], I32, align_bytes=64)
            nc.vector.tensor_copy(
                out=w1_sorted[:].rearrange("p t b m -> p (t b m)").rearrange("p (t q i) -> p q t i", t=PACK, i=4),
                in_=w1_raw_tiles[(e, chunk)][:].rearrange("p g n -> p (g n)").rearrange("p (q i t) -> p q t i", t=PACK, i=4),
            )
            for c in range(first, first + passes):
                for g in range(H_PASSES):
                    for t in range(PACK):
                        w1_sorted_tiles[(e, c, g, t)] = w1_sorted[:, t, passes * g + c - first, :]

        x_grouped_tiles = {}
        x_mx = {}

        def transpose_x(e):
            x_words = x_tiles[e][:].bitcast(F32)
            grouped = x_grouped_pool.tile([P, H_PASSES, TOK_TILES, P, PACK], BF16, align_bytes=64)
            for j in range(TOK_TILES):
                bank = psum.tile([P, H_PASSES * 2, P], F32, tag="bank")
                for g in range(H_PASSES):
                    for u in range(2):
                        first = K_PASS // 2 * g
                        nc.tensor.transpose(bank[:, 2 * g + u, :], x_words[:, j, first + u : first + K_PASS // 2 : 2], ident_f32[:])
                nc.scalar.copy(
                    out=grouped[:].bitcast(F32)[:, :, j, :, :],
                    in_=bank[:].rearrange("p (g u) w -> p g w u", u=2),
                )
            x_grouped_tiles[e] = grouped

        def quantise_x(e):
            x_codes = x_mx_pool.tile([P, H_PASSES * C], U32, align_bytes=64)
            x_scales = x_mx_pool.tile([P, H_PASSES * C], U8, align_bytes=64)
            nc.vector.quantize_mx(
                out=x_codes[:].bitcast(FP8X4),
                scales=x_scales[:],
                in_=x_grouped_tiles[e][:].rearrange("p g j w t -> p (g j w t)"),
            )
            x_mx[e] = (x_codes, x_scales)

        h_tiles = {}

        def stage1(e, c):
            x_codes, x_scales = x_mx[e]
            h_rows = h_pool.tile([P, PACK, C], BF16)
            for half in range(2):
                bank = psum.tile([P, 2, C], F32, tag="bank")
                for s in range(2):
                    t = 2 * half + s
                    for g in range(H_PASSES):
                        a, i = divmod(H_PASSES * e + g, PLANES)
                        nc.tensor.matmul_mx(
                            out=bank[:, s, :],
                            lhsT=w1_sorted_tiles[(e, c, g, t)].bitcast(FP8X4),
                            lhsT_scale=w1_planes[4 * i : P, a, K_PASS * c + P * t : K_PASS * c + P * (t + 1)],
                            rhs=x_codes[:, C * g : C * (g + 1)].bitcast(FP8X4),
                            rhs_scale=x_scales[:, C * g : C * (g + 1)],
                            start=(g == 0),
                            stop=(g == H_PASSES - 1),
                        )
                for s in range(2):
                    t = 2 * half + s
                    nc.scalar.activation(
                        out=h_rows[:, t, :],
                        in_=bank[:, s, :],
                        func=GELU,
                        bias=b1_cols[:, t, I_PASSES * e + c : I_PASSES * e + c + 1],
                    )
            h_tiles[(e, c)] = h_rows

        h_grouped_tiles = {}
        h_mx = {}

        def interleave_h(e, c):
            grouped = h_grouped_pool.tile([P, C, PACK], BF16, align_bytes=64)
            if c in SCALAR_INTERLEAVES:
                nc.scalar.copy(out=grouped[:], in_=h_tiles[(e, c)][:].rearrange("p t w -> p w t"))
            else:
                nc.vector.tensor_copy(out=grouped[:], in_=h_tiles[(e, c)][:].rearrange("p t w -> p w t"))
            h_grouped_tiles[(e, c)] = grouped

        def quantise_h(e, c):
            if c == 0:
                h_codes = h_mx_pool.tile([P, I_PASSES * C], U32, align_bytes=64)
                h_scales = h_mx_pool.tile([P, I_PASSES * C], U8, align_bytes=64)
                h_mx[e] = (h_codes, h_scales)
            h_codes, h_scales = h_mx[e]
            nc.vector.quantize_mx(
                out=h_codes[:, C * c : C * (c + 1)].bitcast(FP8X4),
                scales=h_scales[:, C * c : C * (c + 1)],
                in_=h_grouped_tiles[(e, c)][:].rearrange("p w t -> p (w t)"),
            )

        out_tiles = {}

        def stage2(e, j, n):
            if e not in out_tiles:
                out_sb = w1_out_pool.tile([P, TOK_TILES, H], F32, tag="w1_or_out", align_bytes=64)
                out_tiles[e] = out_sb
            out_sb = out_tiles[e]
            h_codes, h_scales = h_mx[e]
            out_rows = out[C * e : C * (e + 1), :].rearrange("(p j) n -> p j n", j=TOK_TILES)
            cols = slice(N_TILE * n, N_TILE * (n + 1))
            acc = psum.tile([P, N_TILE], F32, tag="bank")
            for c in range(I_PASSES):
                tokens = slice(C * c + P * j, C * c + P * (j + 1))
                nc.tensor.matmul_mx(
                    out=acc[:],
                    lhsT=h_codes[:, tokens].bitcast(FP8X4),
                    lhsT_scale=h_scales[:, tokens],
                    rhs=w2_tiles[(e, c, n)].bitcast(FP8X4),
                    rhs_scale=w2_planes[4 * c : P, e, cols],
                    start=(c == 0),
                    stop=(c == I_PASSES - 1),
                )
            nc.vector.tensor_tensor(out=out_sb[:, j, cols], in0=acc[:], in1=b2_all[:, e, cols], op=ADD)
            if e == E - 1:
                nc.sync.dma_start(out=out_rows[:, j, cols], in_=out_sb[:, j, cols])
            elif n == OUT_TILES - 1:
                nc.sync.dma_start(out=out_rows[:, j, :], in_=out_sb[:, j, :])

        def finish_h(e, half):
            for c in (2 * half, 2 * half + 1):
                interleave_h(e, c)
            for c in (2 * half, 2 * half + 1):
                quantise_h(e, c)

        def stage1_chunk(e, chunk):
            first, passes = w1_chunks(e)[chunk]
            for c in range(first, first + passes):
                stage1(e, c)

        def stage2_chunk(e, half):
            for other in range(2):
                if e == E - 1:
                    stage2(e, other, half)
                else:
                    stage2(e, half, other)

        transpose_x(0)
        turn_b1()
        spread_b2(0)
        spread_b2(1)
        sort_planes(0, 0)
        quantise_x(0)
        sort_w1(0, 0)
        stage1_chunk(0, 0)
        sort_w1(0, 1)
        stage1_chunk(0, 1)
        sort_planes(0, 1)
        sort_w1(0, 2)
        transpose_x(1)
        stage1_chunk(0, 2)
        finish_h(0, 0)
        quantise_x(1)
        sort_w1(1, 0)
        stage1_chunk(1, 0)
        finish_h(0, 1)
        sort_w1(1, 1)
        transpose_x(2)
        stage1_chunk(1, 1)
        finish_h(1, 0)
        quantise_x(2)
        sort_planes(1, 0)
        sort_planes(1, 1)
        spread_b2(2)
        spread_b2(3)
        finish_h(1, 1)
        for e in range(E):
            ahead = e + 2
            stage2_chunk(e, 0)
            if ahead < E:
                sort_w1(ahead, 0)
            stage2_chunk(e, 1)
            if ahead < E:
                sort_w1(ahead, 1)
                stage1_chunk(ahead, 0)
                stage1_chunk(ahead, 1)
                finish_h(ahead, 0)
                if ahead + 1 < E:
                    transpose_x(ahead + 1)
                finish_h(ahead, 1)
                if ahead + 1 < E:
                    quantise_x(ahead + 1)
